import numpy as np
import ml_dtypes


def mxq(x, axis, fmt="e4m3"):
    dtype, down = {"e4m3": (ml_dtypes.float8_e4m3fn, 7), "e5m2": (ml_dtypes.float8_e5m2, 14)}[fmt]
    v = np.moveaxis(np.asarray(x, np.float32).astype(ml_dtypes.bfloat16).astype(np.float64), axis, -1)
    blocks = v.reshape(v.shape[:-1] + (-1, 32))
    amax = np.abs(blocks).max(-1, keepdims=True)
    byte = np.maximum(np.where(amax > 0, np.frexp(amax)[1] - 1 + 127, 0) - down, 1)
    scale = np.exp2(byte - 127.0)
    codes = (blocks / scale).astype(np.float32).astype(dtype).astype(np.float64)
    return np.moveaxis((codes * scale).reshape(v.shape), -1, axis)


WIDE = False


def mx_kscale(k):
    if not WIDE:
        return np.ones(k)
    levels = np.array([10, -10, 5, -5, 0])
    a = np.random.permutation(np.resize(levels, k // 512 * 4)).reshape(k // 512, 4)
    idx = np.arange(k)
    return np.exp2(a[idx // 512, idx % 128 // 32])


BF16 = ml_dtypes.bfloat16


def bf(x):
    return np.asarray(x, np.float32).astype(BF16)


def f64(x):
    return np.asarray(x).astype(np.float64)


B, S, D, M, R = 128, 16, 2048, 8, 1024
LN_EPS = 1e-5


def sigmoid(v):
    return 1.0 / (1.0 + np.exp(-v))


def layer_norm(x):
    mu = np.mean(x, axis=-1, keepdims=True)
    var = np.var(x, axis=-1, keepdims=True)
    return (x - mu) / np.sqrt(var + LN_EPS)


def setup_inputs():
    s, t = mx_kscale(D), mx_kscale(R)
    return {"interface": bf(np.random.standard_normal((B, S, D)) * np.sqrt(S) * s),
            "memory": bf(0.5 + np.random.standard_normal((B, M, D))),
            "W_write_key": bf(np.random.standard_normal((R, D)) / np.sqrt(D) / s[None, :] * t[:, None]),
            "W_write_erase": bf(np.random.standard_normal((D, R)) * 1.5 / np.sqrt(R) / t[None, :]),
            "W_write_add": bf(np.random.standard_normal((D, R)) / np.sqrt(R) / t[None, :])}


def reference(interface, memory, W_write_key, W_write_erase, W_write_add):
    i_mean = np.mean(f64(interface), axis=1)
    i_proj = mxq(i_mean, 1, "e4m3") @ mxq(f64(W_write_key), 1, "e4m3").T
    pq = mxq(i_proj, 1, "e4m3")
    erase = sigmoid(pq @ mxq(f64(W_write_erase), 1, "e4m3").T)[:, None, :]
    add = (pq @ mxq(f64(W_write_add), 1, "e4m3").T)[:, None, :]
    return layer_norm(f64(memory) * (1.0 - erase) + add)

@@ -1,0 +1,359 @@
+from contextlib import ExitStack
+
+import concourse.masks as masks
+import concourse.mybir as mybir
+
+FLOPS = 2 * 128 * 2048 * 1024 * 3
+
+F32 = mybir.dt.float32
+BF16 = mybir.dt.bfloat16
+U32 = mybir.dt.uint32
+U8 = mybir.dt.uint8
+FP8X4 = mybir.dt.float8_e4m3fn_x4
+ALU = mybir.AluOpType
+ACT = mybir.ActivationFunctionType
+
+P = 128
+D = 2048
+R = 1024
+M = 8
+LN_EPS = 1e-5
+
+RAW_BUFS = 5
+GRP_BUFS = 4
+W2C_BUFS = 6
+LAG = 2
+BUDGET = 2
+P4_ENG = "gggggggv"
+
+
+def tile_ultralightweightmemory_pa_kernel(
+    tc, interface, memory, W_write_key, W_write_erase, W_write_add, out
+):
+    nc = tc.nc
+    with ExitStack() as ctx:
+        const = ctx.enter_context(tc.tile_pool(name="const", bufs=1))
+        keep = ctx.enter_context(tc.tile_pool(name="keep", bufs=1))
+        rawp = ctx.enter_context(tc.tile_pool(name="rawp", bufs=RAW_BUFS))
+        grpp = ctx.enter_context(tc.tile_pool(name="grpp", bufs=GRP_BUFS))
+        w2cp = ctx.enter_context(tc.tile_pool(name="w2cp", bufs=W2C_BUFS))
+        ps_acc = ctx.enter_context(tc.psum_pool(name="ps_acc", bufs=4))
+        ps_tp = ctx.enter_context(tc.psum_pool(name="ps_tp", bufs=4))
+        ctx.enter_context(tc.manual_schedule())
+
+        x_v = interface.rearrange("b s d -> (b s) d").rearrange("(T p i) d -> T p (i d)", p=P, i=2)
+        wk_v = W_write_key.rearrange("(j p e) d -> j p (e d)", p=P, e=2)
+        w2_v = {
+            "e": W_write_erase.rearrange("(I h p c) r -> I p h (c r)", h=2, p=P, c=2),
+            "a": W_write_add.rearrange("(I h p c) r -> I p h (c r)", h=2, p=P, c=2),
+        }
+        mem_v = memory.rearrange("b m n -> b (m n)")
+        out_v = out.rearrange("b m n -> b (m n)")
+
+        mem_sb = keep.tile([P, M * D], BF16)
+        y = keep.tile([P, M * D], F32)
+        g_sb = keep.tile([P, D], F32)
+        junk = keep.tile([P, D], BF16)
+        ck = keep.tile([P, 4096], U32, align_bytes=64)
+        sk = keep.tile([P, 4096], U8, align_bytes=64)
+        gm = keep.tile([P, 2048], BF16, align_bytes=64)
+        cm = keep.tile([P, 512], U32, align_bytes=64)
+        sm = keep.tile([P, 512], U8, align_bytes=64)
+        gp = keep.tile([P, 1024], BF16, align_bytes=64)
+        cp = keep.tile([P, 256], U32, align_bytes=64)
+        sp = keep.tile([P, 256], U8, align_bytes=64)
+        s4 = keep.tile([P, M, 4], F32)
+        negs = keep.tile([P, M], F32)
+        nm = keep.tile([P, M], F32)
+        q = keep.tile([P, M], F32)
+        sd = keep.tile([P, M], F32)
+        rstd = keep.tile([P, M], F32)
+        warm = keep.tile([P, 2], F32)
+
+        first = [("x", 0), ("x", 1), ("x", 2), ("x", 3), ("k", 0), ("x", 4), ("k", 1), ("x", 5), ("k", 2)]
+        first += [("x", 6), ("x", 7), ("k", 3)]
+        order = list(first)
+        for I in range(4):
+            order += [("e", I), ("m", I)]
+        order += [("a", I) for I in range(4)]
+        state = {"next": 0}
+        raw = {}
+
+        def advance():
+            while state["next"] < len(order):
+                kind, idx = order[state["next"]]
+                state["next"] += 1
+                if kind == "m":
+                    nc.sync.dma_start(
+                        out=mem_sb[:, 4096 * idx : 4096 * (idx + 1)],
+                        in_=mem_v[:, 4096 * idx : 4096 * (idx + 1)],
+                    )
+                    continue
+                t = rawp.tile([P, 4096], BF16, tag="raw", name="raw_%s%d" % (kind, idx))
+                if kind == "k":
+                    nc.sync.dma_start(out=t[:], in_=wk_v[idx])
+                elif kind == "x":
+                    nc.sync.dma_start(out=t[:], in_=x_v[idx])
+                else:
+                    nc.sync.dma_start(out=t[:].rearrange("p (h x) -> p h x", h=2), in_=w2_v[kind][idx])
+                raw[(kind, idx)] = t
+                return
+
+        for n in range(RAW_BUFS):
+            advance()
+
+        ident_f = const.tile([P, P], F32)
+        masks.make_identity(nc, ident_f[:])
+        ident_b = const.tile([P, P], BF16)
+        masks.make_identity(nc, ident_b[:])
+        r32 = const.tile([P, 16], F32)
+        nc.vector.tensor_reduce(
+            out=r32[:], in_=ident_f[:].rearrange("p (n s) -> p n s", s=8), axis=mybir.AxisListType.X, op=ALU.add
+        )
+        r16 = const.tile([P, 16], BF16)
+        nc.vector.tensor_scalar_mul(out=r16[:], in0=r32[:], scalar1=1.0 / 16.0)
+        eps = const.tile([P, 1], F32)
+        nc.vector.memset(eps[:], LN_EPS)
+        nc.scalar.activation(out=warm[:, 0:1], in_=eps[:], func=ACT.Sigmoid)
+
+        def evac(eng, dst, src):
+            if eng == "v":
+                nc.vector.tensor_copy(out=dst, in_=src)
+            else:
+                nc.scalar.copy(out=dst, in_=src)
+
+        pending = []
+
+        def later(fn):
+            pending.append(fn)
+            if len(pending) > 1:
+                pending.pop(0)()
+
+        def flush():
+            while pending:
+                pending.pop(0)()
+
+        def quant(codes_ap, scales_ap, in_ap):
+            nc.vector.quantize_mx(out=codes_ap.bitcast(FP8X4), scales=scales_ap, in_=in_ap)
+
+        def kunit(j, e):
+            rk = raw[("k", j)]
+            ce = 2 * j + e
+            gk = grpp.tile([P, 2048], BF16, tag="grp", name="gk%d" % ce, align_bytes=64)
+            for g in range(4):
+                tp = ps_tp.tile([P, 4, P], BF16, tag="tp", name="tpk%d_%d" % (ce, g))
+                for t in range(4):
+                    d0 = e * D + 512 * g + 128 * t
+                    nc.tensor.transpose(tp[:, t, :], rk[:, d0 : d0 + 128], ident_b[:])
+                evac(
+                    "vs"[g % 2],
+                    gk[:, 512 * g : 512 * (g + 1)].rearrange("p (c t) -> p c t", t=4),
+                    tp[:].rearrange("p t c -> p c t"),
+                )
+            later(lambda: quant(ck[:, 512 * ce : 512 * (ce + 1)], sk[:, 512 * ce : 512 * (ce + 1)], gk[:]))
+
+        mean_ps = [ps_acc.tile([P, 4, P], F32, tag="acc", name="mean%d" % g) for g in range(4)]
+
+        def mean_unit(T):
+            xt = raw[("x", T)]
+            for c in range(16):
+                for i in range(2):
+                    nc.tensor.matmul(
+                        mean_ps[c // 4][:, c % 4, 16 * T : 16 * (T + 1)],
+                        lhsT=xt[:, i * D + 128 * c : i * D + 128 * (c + 1)],
+                        rhs=r16[:],
+                        start=(i == 0),
+                        stop=(i == 1),
+                    )
+
+        def mean_out():
+            for g in range(4):
+                evac(
+                    "vs"[g % 2],
+                    gm[:, 512 * g : 512 * (g + 1)].rearrange("p (b t) -> p b t", t=4),
+                    mean_ps[g][:].rearrange("p t b -> p b t"),
+                )
+                if g == 2:
+                    quant(cm[:, 0:256], sm[:, 0:256], gm[:, 0:1024])
+            quant(cm[:, 256:512], sm[:, 256:512], gm[:, 1024:2048])
+
+        for kind, idx in first:
+            if kind == "x":
+                mean_unit(idx)
+            else:
+                kunit(idx, 0)
+                kunit(idx, 1)
+            advance()
+            if (kind, idx) == ("x", 7):
+                flush()
+                mean_out()
+        flush()
+
+        w2 = [("e", I, h) for I in range(4) for h in range(2)] + [("a", I, h) for I in range(4) for h in range(2)]
+        codes = {}
+
+        def prep(idx):
+            kind, I, h = w2[idx]
+            rwf = raw[(kind, I)][:].bitcast(F32)
+            gw = grpp.tile([P, 2048], BF16, tag="grp", name="gw%d" % idx, align_bytes=64)
+            gwf = gw[:].bitcast(F32)
+            for G in range(2):
+                tp = ps_tp.tile([P, 2, 2, P], F32, tag="tp", name="tpw%d_%d" % (idx, G))
+                for c in range(2):
+                    for u in range(2):
+                        w0 = (h * 2 + c) * 512 + 256 * G + 128 * u
+                        nc.tensor.transpose(tp[:, c, u, :], rwf[:, w0 : w0 + 128], ident_f[:])
+                evac(
+                    "s",
+                    gwf[:, 512 * G : 512 * (G + 1)].rearrange("q (p c u) -> q p c u", c=2, u=2),
+                    tp[:].rearrange("q c u p -> q p c u"),
+                )
+            if h == 1:
+                advance()
+            cw = w2cp.tile([P, 512], U32, tag="cw", name="cw%d" % idx, align_bytes=64)
+            sw = w2cp.tile([P, 512], U8, tag="sw", name="sw%d" % idx, align_bytes=64)
+            codes[idx] = (cw, sw)
+            later(lambda: quant(cw[:], sw[:], gw[:]))
+
+        pj = {}
+
+        def stage1(ce):
+            G, t = divmod(ce, 4)
+            if t == 0:
+                pj[G] = ps_tp.tile([P, 4, P], F32, tag="tp", name="pj%d" % G)
+            for g in range(4):
+                lo = 512 * ce + 128 * g
+                nc.tensor.matmul_mx(
+                    out=pj[G][:, t, :],
+                    lhsT=ck[:, lo : lo + 128].bitcast(FP8X4),
+                    lhsT_scale=sk[:, lo : lo + 128],
+                    rhs=cm[:, 128 * g : 128 * (g + 1)].bitcast(FP8X4),
+                    rhs_scale=sm[:, 128 * g : 128 * (g + 1)],
+                    start=(g == 0),
+                    stop=(g == 3),
+                )
+            if t == 3:
+                evac(
+                    "vs"[G],
+                    gp[:, 512 * G : 512 * (G + 1)].rearrange("p (b t) -> p b t", t=4),
+                    pj[G][:].rearrange("p t b -> p b t"),
+                )
+
+        for ce in range(8):
+            stage1(ce)
+            if ce == 5:
+                quant(cp[:, 0:128], sp[:, 0:128], gp[:, 0:512])
+        quant(cp[:, 128:256], sp[:, 128:256], gp[:, 512:1024])
+        prep(0)
+        prep(1)
+        prep(2)
+
+        acc = {}
+        yv = y[:].rearrange("p (m n) -> p m n", m=M)
+        mv = mem_sb[:].rearrange("p (m n) -> p m n", m=M)
+        ready = []
+        queued = set()
+        chunks_done = []
+
+        def gate(pair0, pair1, c):
+            ms = slice(2 * pair0, 2 * pair1 + 2)
+            ns = slice(512 * c, 512 * (c + 1))
+            nc.vector.tensor_tensor(
+                out=yv[:, ms, ns],
+                in0=mv[:, ms, ns],
+                in1=g_sb[:, ns].unsqueeze(1).to_broadcast([P, 2 * (pair1 - pair0 + 1), 512]),
+                op=ALU.mult,
+            )
+
+        def filler(step, budget):
+            for c in chunks_done:
+                for pair in range(4):
+                    if 2 * pair + 2 <= step and (pair, c) not in queued:
+                        queued.add((pair, c))
+                        ready.append((pair, c))
+            take = [ready.pop(0) for n in range(min(budget, len(ready)))]
+            while take:
+                pair, c = take.pop(0)
+                if take and take[0] == (pair + 1, c):
+                    take.pop(0)
+                    gate(pair, pair + 1, c)
+                else:
+                    gate(pair, pair, c)
+
+        def mult(idx):
+            kind, I, h = w2[idx]
+            if h == 0:
+                acc[(kind, I)] = ps_acc.tile([P, 512], F32, tag="acc", name="o_%s%d" % (kind, I))
+            o_ps = acc[(kind, I)]
+            cw, sw = codes[idx]
+            for G in range(2):
+                nc.tensor.matmul_mx(
+                    out=o_ps[:, 256 * h : 256 * (h + 1)],
+                    lhsT=cp[:, 128 * G : 128 * (G + 1)].bitcast(FP8X4),
+                    lhsT_scale=sp[:, 128 * G : 128 * (G + 1)],
+                    rhs=cw[:, 256 * G : 256 * (G + 1)].bitcast(FP8X4),
+                    rhs_scale=sw[:, 256 * G : 256 * (G + 1)],
+                    start=(G == 0),
+                    stop=(G == 1),
+                )
+            if h == 0:
+                return
+            cols = slice(512 * I, 512 * (I + 1))
+            if kind == "e":
+                nc.scalar.activation(out=g_sb[:, cols], in_=o_ps[:], func=ACT.Sigmoid, scale=-1.0)
+                chunks_done.append(I)
+                if I == 3:
+                    nc.scalar.activation(out=warm[:, 1:2], in_=g_sb[:, D - 1 : D], func=ACT.Sqrt)
+
+        mult(0)
+        mult(1)
+        filler(3, BUDGET)
+        for idx in range(3, len(w2) + LAG):
+            if idx < len(w2):
+                prep(idx)
+            else:
+                flush()
+            if idx - LAG >= 2:
+                mult(idx - LAG)
+            filler(idx, BUDGET)
+        filler(99, 99)
+
+        def add_slot(m):
+            for I in range(4):
+                ym = y[:, D * m + 512 * I : D * m + 512 * (I + 1)]
+                nc.vector.scalar_tensor_tensor(
+                    out=ym,
+                    in0=ym,
+                    scalar=1.0,
+                    in1=acc[("a", I)][:],
+                    op0=ALU.mult,
+                    op1=ALU.add,
+                    accum_out=s4[:, m, I : I + 1],
+                )
+            nc.vector.tensor_reduce(
+                out=negs[:, m : m + 1], in_=s4[:, m, :], axis=mybir.AxisListType.X, op=ALU.add, negate=True
+            )
+            nc.gpsimd.tensor_scalar(
+                out=nm[:, m : m + 1], in0=negs[:, m : m + 1], scalar1=1.0 / D, scalar2=0.0, op0=ALU.mult, op1=ALU.add
+            )
+
+        add_slot(0)
+        for m in range(M):
+            if m + 1 < M:
+                add_slot(m + 1)
+            ym = y[:, D * m : D * (m + 1)]
+            col = slice(m, m + 1)
+            nc.scalar.activation(
+                out=junk[:], in_=ym, func=ACT.Square, bias=negs[:, col], scale=float(D), accum_out=q[:, col]
+            )
+            nc.scalar.activation(out=sd[:, col], in_=q[:, col], func=ACT.Sqrt, bias=eps[:], scale=1.0 / (D * D * D))
+            nc.vector.reciprocal(out=rstd[:, col], in_=sd[:, col])
+            if P4_ENG[m] == "v":
+                nc.vector.tensor_scalar(
+                    out=ym, in0=ym, scalar1=nm[:, col], scalar2=rstd[:, col], op0=ALU.add, op1=ALU.mult
+                )
+            else:
+                nc.gpsimd.tensor_scalar(
+                    out=ym, in0=ym, scalar1=nm[:, col], scalar2=rstd[:, col], op0=ALU.add, op1=ALU.mult
+                )
+            nc.sync.dma_start(out=out_v[:, D * m : D * (m + 1)], in_=ym)

@@ -19,12 +19,17 @@ R = 1024
 M = 8
 LN_EPS = 1e-5
 
-RAW_BUFS = 5
+RAW_BUFS = 7
 GRP_BUFS = 4
-W2C_BUFS = 6
+W2C_BUFS = 4
+PRE = 2
 LAG = 2
-BUDGET = 2
-P4_ENG = "gggggggv"
+GLAG = 1
+EV = "ssv"
+GSLOTS = [4, 5, 6, 7]
+G_LATE = []
+P4 = "ggggggvv"
+TAPER = 4
 
 
 def tile_ultralightweightmemory_pa_kernel(
@@ -36,6 +41,7 @@ def tile_ultralightweightmemory_pa_kernel(
         keep = ctx.enter_context(tc.tile_pool(name="keep", bufs=1))
         rawp = ctx.enter_context(tc.tile_pool(name="rawp", bufs=RAW_BUFS))
         grpp = ctx.enter_context(tc.tile_pool(name="grpp", bufs=GRP_BUFS))
+        gtp = ctx.enter_context(tc.tile_pool(name="gtp", bufs=2))
         w2cp = ctx.enter_context(tc.tile_pool(name="w2cp", bufs=W2C_BUFS))
         ps_acc = ctx.enter_context(tc.psum_pool(name="ps_acc", bufs=4))
         ps_tp = ctx.enter_context(tc.psum_pool(name="ps_tp", bufs=4))
@@ -70,24 +76,17 @@ def tile_ultralightweightmemory_pa_kernel(
         rstd = keep.tile([P, M], F32)
         warm = keep.tile([P, 2], F32)
 
-        first = [("x", 0), ("x", 1), ("x", 2), ("x", 3), ("k", 0), ("x", 4), ("k", 1), ("x", 5), ("k", 2)]
-        first += [("x", 6), ("x", 7), ("k", 3)]
-        order = list(first)
-        for I in range(4):
-            order += [("e", I), ("m", I)]
-        order += [("a", I) for I in range(4)]
-        state = {"next": 0}
+        order = [("k", i) for i in range(4)] + [("x", i) for i in range(8)] + [("e", i) for i in range(4)]
+        order += [("a", i) for i in range(4)] + [("m", i) for i in range(M)]
+        state = {"pos": 0}
         raw = {}
 
         def advance():
-            while state["next"] < len(order):
-                kind, idx = order[state["next"]]
-                state["next"] += 1
+            while state["pos"] < len(order):
+                kind, idx = order[state["pos"]]
+                state["pos"] += 1
                 if kind == "m":
-                    nc.sync.dma_start(
-                        out=mem_sb[:, 4096 * idx : 4096 * (idx + 1)],
-                        in_=mem_v[:, 4096 * idx : 4096 * (idx + 1)],
-                    )
+                    nc.sync.dma_start(out=mem_sb[:, D * idx : D * (idx + 1)], in_=mem_v[:, D * idx : D * (idx + 1)])
                     continue
                 t = rawp.tile([P, 4096], BF16, tag="raw", name="raw_%s%d" % (kind, idx))
                 if kind == "k":
@@ -122,19 +121,14 @@ def tile_ultralightweightmemory_pa_kernel(
             else:
                 nc.scalar.copy(out=dst, in_=src)
 
-        pending = []
-
-        def later(fn):
-            pending.append(fn)
-            if len(pending) > 1:
-                pending.pop(0)()
-
-        def flush():
-            while pending:
-                pending.pop(0)()
-
         def quant(codes_ap, scales_ap, in_ap):
             nc.vector.quantize_mx(out=codes_ap.bitcast(FP8X4), scales=scales_ap, in_=in_ap)
+
+        quants = []
+
+        def do_quants(keep_back):
+            while len(quants) > keep_back:
+                quants.pop(0)()
 
         def kunit(j, e):
             rk = raw[("k", j)]
@@ -150,7 +144,8 @@ def tile_ultralightweightmemory_pa_kernel(
                     gk[:, 512 * g : 512 * (g + 1)].rearrange("p (c t) -> p c t", t=4),
                     tp[:].rearrange("p t c -> p c t"),
                 )
-            later(lambda: quant(ck[:, 512 * ce : 512 * (ce + 1)], sk[:, 512 * ce : 512 * (ce + 1)], gk[:]))
+            quants.append(lambda: quant(ck[:, 512 * ce : 512 * (ce + 1)], sk[:, 512 * ce : 512 * (ce + 1)], gk[:]))
+            do_quants(1)
 
         mean_ps = [ps_acc.tile([P, 4, P], F32, tag="acc", name="mean%d" % g) for g in range(4)]
 
@@ -177,19 +172,10 @@ def tile_ultralightweightmemory_pa_kernel(
                     quant(cm[:, 0:256], sm[:, 0:256], gm[:, 0:1024])
             quant(cm[:, 256:512], sm[:, 256:512], gm[:, 1024:2048])
 
-        for kind, idx in first:
-            if kind == "x":
-                mean_unit(idx)
-            else:
-                kunit(idx, 0)
-                kunit(idx, 1)
-            advance()
-            if (kind, idx) == ("x", 7):
-                flush()
-                mean_out()
-        flush()
-
-        w2 = [("e", I, h) for I in range(4) for h in range(2)] + [("a", I, h) for I in range(4) for h in range(2)]
+        w2 = []
+        for kind, idx in order:
+            if kind in "ea":
+                w2 += [(kind, idx, 0), (kind, idx, 1)]
         codes = {}
 
         def prep(idx):
@@ -204,16 +190,35 @@ def tile_ultralightweightmemory_pa_kernel(
                         w0 = (h * 2 + c) * 512 + 256 * G + 128 * u
                         nc.tensor.transpose(tp[:, c, u, :], rwf[:, w0 : w0 + 128], ident_f[:])
                 evac(
-                    "s",
+                    EV[(2 * idx + G) % len(EV)],
                     gwf[:, 512 * G : 512 * (G + 1)].rearrange("q (p c u) -> q p c u", c=2, u=2),
                     tp[:].rearrange("q c u p -> q p c u"),
                 )
             if h == 1:
                 advance()
-            cw = w2cp.tile([P, 512], U32, tag="cw", name="cw%d" % idx, align_bytes=64)
-            sw = w2cp.tile([P, 512], U8, tag="sw", name="sw%d" % idx, align_bytes=64)
-            codes[idx] = (cw, sw)
-            later(lambda: quant(cw[:], sw[:], gw[:]))
+            if kind == "e":
+                cw = w2cp.tile([P, 512], U32, tag="cw", name="cw%d" % idx, align_bytes=64)
+                sw = w2cp.tile([P, 512], U8, tag="sw", name="sw%d" % idx, align_bytes=64)
+                codes[idx] = (cw[:], sw[:])
+            else:
+                i = 2 * I + h
+                codes[idx] = (ck[:, 512 * i : 512 * (i + 1)], sk[:, 512 * i : 512 * (i + 1)])
+            cwa, swa = codes[idx]
+            quants.append(lambda: quant(cwa, swa, gw[:]))
+
+        for kind, idx in order:
+            if kind == "x":
+                mean_unit(idx)
+                advance()
+            elif kind == "k":
+                kunit(idx, 0)
+                kunit(idx, 1)
+                advance()
+        do_quants(0)
+        mean_out()
+        for z in range(PRE):
+            prep(z)
+            do_quants(1)
 
         pj = {}
 
@@ -234,7 +239,7 @@ def tile_ultralightweightmemory_pa_kernel(
                 )
             if t == 3:
                 evac(
-                    "vs"[G],
+                    "v",
                     gp[:, 512 * G : 512 * (G + 1)].rearrange("p (b t) -> p b t", t=4),
                     pj[G][:].rearrange("p t b -> p b t"),
                 )
@@ -243,80 +248,102 @@ def tile_ultralightweightmemory_pa_kernel(
             stage1(ce)
             if ce == 5:
                 quant(cp[:, 0:128], sp[:, 0:128], gp[:, 0:512])
+                do_quants(0)
         quant(cp[:, 128:256], sp[:, 128:256], gp[:, 512:1024])
-        prep(0)
-        prep(1)
-        prep(2)
 
-        acc = {}
+        def proj(G):
+            return cp[:, 128 * G : 128 * (G + 1)].bitcast(FP8X4), sp[:, 128 * G : 128 * (G + 1)]
+
+        gT = {}
+        gps = {}
+
+        def zt(I):
+            z = ps_tp.tile([P, 4, P], F32, tag="tp", name="zt%d" % I)
+            for h in range(2):
+                cw, sw = codes[2 * I + h]
+                for j in range(2):
+                    for G in range(2):
+                        lo = 256 * G + 128 * j
+                        pc, ps = proj(G)
+                        nc.tensor.matmul_mx(
+                            out=z[:, 2 * h + j, :],
+                            lhsT=cw[:, lo : lo + 128].bitcast(FP8X4),
+                            lhsT_scale=sw[:, lo : lo + 128],
+                            rhs=pc,
+                            rhs_scale=ps,
+                            start=(G == 0),
+                            stop=(G == 1),
+                        )
+            gT[I] = gtp.tile([P, 512], F32, tag="gT", name="gT%d" % I)
+            nc.scalar.activation(out=gT[I][:], in_=z[:].rearrange("p j b -> p (j b)"), func=ACT.Sigmoid, scale=-1.0)
+            zn = ps_tp.tile([P, 512], F32, tag="tp", name="zn%d" % I)
+            second(zn, 2 * I)
+            nc.scalar.activation(out=g_sb[:, 512 * I : 512 * (I + 1)], in_=zn[:], func=ACT.Sigmoid, scale=-1.0)
+
+        def second(o_ps, idx0):
+            for h in range(2):
+                cw, sw = codes[idx0 + h]
+                for G in range(2):
+                    pc, ps = proj(G)
+                    nc.tensor.matmul_mx(
+                        out=o_ps[:, 256 * h : 256 * (h + 1)],
+                        lhsT=pc,
+                        lhsT_scale=ps,
+                        rhs=cw[:, 256 * G : 256 * (G + 1)].bitcast(FP8X4),
+                        rhs_scale=sw[:, 256 * G : 256 * (G + 1)],
+                        start=(G == 0),
+                        stop=(G == 1),
+                    )
+
+        def gtrans(I):
+            gps[I] = ps_acc.tile([P, 512], F32, tag="acc", name="gps%d" % I)
+            for jj in range(4):
+                nc.tensor.transpose(gps[I][:, 128 * jj : 128 * (jj + 1)], gT[I][:, 128 * jj : 128 * (jj + 1)], ident_f[:])
+
+        n2 = len(w2)
+        for idx in range(PRE, n2 + LAG + GLAG + 1):
+            if idx < n2:
+                prep(idx)
+                do_quants(1)
+            j = idx - LAG
+            if 0 <= j < 8 and j % 2 == 1:
+                zt(j // 2)
+            j = idx - LAG - GLAG
+            if 0 <= j < 8 and j % 2 == 1:
+                gtrans(j // 2)
+        do_quants(0)
+        nc.scalar.activation(out=warm[:, 1:2], in_=g_sb[:, D - 1 : D], func=ACT.Sqrt)
+
         yv = y[:].rearrange("p (m n) -> p m n", m=M)
         mv = mem_sb[:].rearrange("p (m n) -> p m n", m=M)
-        ready = []
-        queued = set()
-        chunks_done = []
+        vslots = [m for m in range(M) if m not in GSLOTS]
 
-        def gate(pair0, pair1, c):
-            ms = slice(2 * pair0, 2 * pair1 + 2)
+        def gate_v(m0, m1, c):
             ns = slice(512 * c, 512 * (c + 1))
             nc.vector.tensor_tensor(
-                out=yv[:, ms, ns],
-                in0=mv[:, ms, ns],
-                in1=g_sb[:, ns].unsqueeze(1).to_broadcast([P, 2 * (pair1 - pair0 + 1), 512]),
+                out=yv[:, m0 : m1 + 1, ns],
+                in0=mv[:, m0 : m1 + 1, ns],
+                in1=gps[c][:].unsqueeze(1).to_broadcast([P, m1 - m0 + 1, 512]),
                 op=ALU.mult,
             )
 
-        def filler(step, budget):
-            for c in chunks_done:
-                for pair in range(4):
-                    if 2 * pair + 2 <= step and (pair, c) not in queued:
-                        queued.add((pair, c))
-                        ready.append((pair, c))
-            take = [ready.pop(0) for n in range(min(budget, len(ready)))]
-            while take:
-                pair, c = take.pop(0)
-                if take and take[0] == (pair + 1, c):
-                    take.pop(0)
-                    gate(pair, pair + 1, c)
-                else:
-                    gate(pair, pair, c)
+        def gate_g(m):
+            nc.gpsimd.tensor_tensor(
+                out=y[:, D * m : D * (m + 1)], in0=mem_sb[:, D * m : D * (m + 1)], in1=g_sb[:], op=ALU.mult
+            )
 
-        def mult(idx):
-            kind, I, h = w2[idx]
-            if h == 0:
-                acc[(kind, I)] = ps_acc.tile([P, 512], F32, tag="acc", name="o_%s%d" % (kind, I))
-            o_ps = acc[(kind, I)]
-            cw, sw = codes[idx]
-            for G in range(2):
-                nc.tensor.matmul_mx(
-                    out=o_ps[:, 256 * h : 256 * (h + 1)],
-                    lhsT=cp[:, 128 * G : 128 * (G + 1)].bitcast(FP8X4),
-                    lhsT_scale=sp[:, 128 * G : 128 * (G + 1)],
-                    rhs=cw[:, 256 * G : 256 * (G + 1)].bitcast(FP8X4),
-                    rhs_scale=sw[:, 256 * G : 256 * (G + 1)],
-                    start=(G == 0),
-                    stop=(G == 1),
-                )
-            if h == 0:
-                return
-            cols = slice(512 * I, 512 * (I + 1))
-            if kind == "e":
-                nc.scalar.activation(out=g_sb[:, cols], in_=o_ps[:], func=ACT.Sigmoid, scale=-1.0)
-                chunks_done.append(I)
-                if I == 3:
-                    nc.scalar.activation(out=warm[:, 1:2], in_=g_sb[:, D - 1 : D], func=ACT.Sqrt)
+        late = [m for i, m in G_LATE]
+        for m in GSLOTS:
+            if m not in late:
+                gate_g(m)
+        for i in range(0, len(vslots), 2):
+            for c in range(4):
+                gate_v(vslots[i], vslots[i + 1], c)
 
-        mult(0)
-        mult(1)
-        filler(3, BUDGET)
-        for idx in range(3, len(w2) + LAG):
-            if idx < len(w2):
-                prep(idx)
-            else:
-                flush()
-            if idx - LAG >= 2:
-                mult(idx - LAG)
-            filler(idx, BUDGET)
-        filler(99, 99)
+        a_ps = []
+        for I in range(4):
+            a_ps.append(ps_tp.tile([P, 512], F32, tag="tp", name="a%d" % I))
+            second(a_ps[I], 8 + 2 * I)
 
         def add_slot(m):
             for I in range(4):
@@ -325,7 +352,7 @@ def tile_ultralightweightmemory_pa_kernel(
                     out=ym,
                     in0=ym,
                     scalar=1.0,
-                    in1=acc[("a", I)][:],
+                    in1=a_ps[I][:],
                     op0=ALU.mult,
                     op1=ALU.add,
                     accum_out=s4[:, m, I : I + 1],
@@ -333,27 +360,34 @@ def tile_ultralightweightmemory_pa_kernel(
             nc.vector.tensor_reduce(
                 out=negs[:, m : m + 1], in_=s4[:, m, :], axis=mybir.AxisListType.X, op=ALU.add, negate=True
             )
-            nc.gpsimd.tensor_scalar(
-                out=nm[:, m : m + 1], in0=negs[:, m : m + 1], scalar1=1.0 / D, scalar2=0.0, op0=ALU.mult, op1=ALU.add
-            )
 
-        add_slot(0)
-        for m in range(M):
-            if m + 1 < M:
-                add_slot(m + 1)
+        border = vslots + GSLOTS
+        add_slot(border[0])
+        for i, m in enumerate(border):
+            if i + 1 < M:
+                add_slot(border[i + 1])
             ym = y[:, D * m : D * (m + 1)]
             col = slice(m, m + 1)
             nc.scalar.activation(
                 out=junk[:], in_=ym, func=ACT.Square, bias=negs[:, col], scale=float(D), accum_out=q[:, col]
             )
             nc.scalar.activation(out=sd[:, col], in_=q[:, col], func=ACT.Sqrt, bias=eps[:], scale=1.0 / (D * D * D))
+            nc.scalar.activation(out=nm[:, col], in_=negs[:, col], func=ACT.Copy, scale=1.0 / D)
             nc.vector.reciprocal(out=rstd[:, col], in_=sd[:, col])
-            if P4_ENG[m] == "v":
-                nc.vector.tensor_scalar(
-                    out=ym, in0=ym, scalar1=nm[:, col], scalar2=rstd[:, col], op0=ALU.add, op1=ALU.mult
-                )
+            if P4[i] == "v":
+                nt = TAPER if i == M - 1 else 1
+                w = D // nt
+                for z in range(nt):
+                    yz = y[:, D * m + w * z : D * m + w * (z + 1)]
+                    nc.vector.tensor_scalar(
+                        out=yz, in0=yz, scalar1=nm[:, col], scalar2=rstd[:, col], op0=ALU.add, op1=ALU.mult
+                    )
+                    nc.sync.dma_start(out=out_v[:, D * m + w * z : D * m + w * (z + 1)], in_=yz)
             else:
                 nc.gpsimd.tensor_scalar(
                     out=ym, in0=ym, scalar1=nm[:, col], scalar2=rstd[:, col], op0=ALU.add, op1=ALU.mult
                 )
-            nc.sync.dma_start(out=out_v[:, D * m : D * (m + 1)], in_=ym)
+                nc.sync.dma_start(out=out_v[:, D * m : D * (m + 1)], in_=ym)
+            for ii, mm in G_LATE:
+                if ii == i:
+                    gate_g(mm)

@@ -16,18 +16,22 @@ ACT = mybir.ActivationFunctionType
 P = 128
 D = 2048
 R = 1024
-M = 8
+L = 4
 LN_EPS = 1e-5
 
-RAW_BUFS = 7
+BIG_SLOT = {"k0": 0, "k1": 1, "x0": 2, "x1": 3, "e0": 4, "e1": 5, "a0": 2, "a1": 3, "x2": 4, "x3": 5, "y00": 0, "y01": 1, "y10": 2, "y11": 3}
+MEAN_AT = [(13, 4),(15, 5),(16, 6)]
+TP2_FROM = 15
+A_BANK = [2, 3, 4, 5]
 GRP_BUFS = 4
-W2C_BUFS = 4
-PRE = 2
+EVE = "ss"
+EVA = "ss"
+A0_FROM = 4
+PRE = 3
 LAG = 2
-GLAG = 1
-EV = "ssv"
-GSLOTS = [4, 5, 6, 7]
-G_LATE = []
+FILL = [0,0,1,0,1,1,1,0,1,1,1,1,1,0,1,0,0,0,0]
+MPOS = 4
+SEQ0 = ["u1","M","u1","p0","p1","u9","z0","z1","f0","z2","f1","z3","f2","f3"]
 P4 = "ggggggvv"
 TAPER = 4
 
@@ -39,13 +43,13 @@ def tile_ultralightweightmemory_pa_kernel(
     with ExitStack() as ctx:
         const = ctx.enter_context(tc.tile_pool(name="const", bufs=1))
         keep = ctx.enter_context(tc.tile_pool(name="keep", bufs=1))
-        rawp = ctx.enter_context(tc.tile_pool(name="rawp", bufs=RAW_BUFS))
+        bigp = ctx.enter_context(tc.tile_pool(name="bigp", bufs=1))
         grpp = ctx.enter_context(tc.tile_pool(name="grpp", bufs=GRP_BUFS))
-        gtp = ctx.enter_context(tc.tile_pool(name="gtp", bufs=2))
-        w2cp = ctx.enter_context(tc.tile_pool(name="w2cp", bufs=W2C_BUFS))
-        ps_acc = ctx.enter_context(tc.psum_pool(name="ps_acc", bufs=4))
-        ps_tp = ctx.enter_context(tc.psum_pool(name="ps_tp", bufs=4))
+        psum = ctx.enter_context(tc.psum_pool(name="psum", bufs=1))
         ctx.enter_context(tc.manual_schedule())
+
+        def bank(n, shape, dtype, name):
+            return psum.tile(shape, dtype, tag="bank%d" % n, name=name)
 
         x_v = interface.rearrange("b s d -> (b s) d").rearrange("(T p i) d -> T p (i d)", p=P, i=2)
         wk_v = W_write_key.rearrange("(j p e) d -> j p (e d)", p=P, e=2)
@@ -53,53 +57,65 @@ def tile_ultralightweightmemory_pa_kernel(
             "e": W_write_erase.rearrange("(I h p c) r -> I p h (c r)", h=2, p=P, c=2),
             "a": W_write_add.rearrange("(I h p c) r -> I p h (c r)", h=2, p=P, c=2),
         }
-        mem_v = memory.rearrange("b m n -> b (m n)")
-        out_v = out.rearrange("b m n -> b (m n)")
+        mem_v = memory.rearrange("b (u l) n -> (b u) (l n)", u=2)
+        out_v = out.rearrange("b (u l) n -> (b u) (l n)", u=2)
 
-        mem_sb = keep.tile([P, M * D], BF16)
-        y = keep.tile([P, M * D], F32)
+        mem_sb = [keep.tile([P, L * D], BF16, name="mem%d" % hf) for hf in range(2)]
         g_sb = keep.tile([P, D], F32)
         junk = keep.tile([P, D], BF16)
-        ck = keep.tile([P, 4096], U32, align_bytes=64)
-        sk = keep.tile([P, 4096], U8, align_bytes=64)
+        cws = {}
+        sws = {}
+        for kind in "kea":
+            cws[kind] = keep.tile([P, 4096], U32, name="c_%s" % kind, align_bytes=64)
+            sws[kind] = keep.tile([P, 4096], U8, name="s_%s" % kind, align_bytes=64)
+        ck = cws["k"]
+        sk = sws["k"]
         gm = keep.tile([P, 2048], BF16, align_bytes=64)
         cm = keep.tile([P, 512], U32, align_bytes=64)
         sm = keep.tile([P, 512], U8, align_bytes=64)
         gp = keep.tile([P, 1024], BF16, align_bytes=64)
         cp = keep.tile([P, 256], U32, align_bytes=64)
         sp = keep.tile([P, 256], U8, align_bytes=64)
-        s4 = keep.tile([P, M, 4], F32)
-        negs = keep.tile([P, M], F32)
-        nm = keep.tile([P, M], F32)
-        q = keep.tile([P, M], F32)
-        sd = keep.tile([P, M], F32)
-        rstd = keep.tile([P, M], F32)
-        warm = keep.tile([P, 2], F32)
+        s4 = keep.tile([P, 2 * L, 4], F32)
+        negs = keep.tile([P, 2 * L], F32)
+        nm = keep.tile([P, 2 * L], F32)
+        q = keep.tile([P, 2 * L], F32)
+        t1 = keep.tile([P, 2 * L], F32)
+        rstd = keep.tile([P, 2 * L], F32)
+        warm = keep.tile([P, 1], F32)
 
-        order = [("k", i) for i in range(4)] + [("x", i) for i in range(8)] + [("e", i) for i in range(4)]
-        order += [("a", i) for i in range(4)] + [("m", i) for i in range(M)]
-        state = {"pos": 0}
         raw = {}
+        big = {}
 
-        def advance():
-            while state["pos"] < len(order):
-                kind, idx = order[state["pos"]]
-                state["pos"] += 1
-                if kind == "m":
-                    nc.sync.dma_start(out=mem_sb[:, D * idx : D * (idx + 1)], in_=mem_v[:, D * idx : D * (idx + 1)])
-                    continue
-                t = rawp.tile([P, 4096], BF16, tag="raw", name="raw_%s%d" % (kind, idx))
-                if kind == "k":
-                    nc.sync.dma_start(out=t[:], in_=wk_v[idx])
-                elif kind == "x":
-                    nc.sync.dma_start(out=t[:], in_=x_v[idx])
-                else:
-                    nc.sync.dma_start(out=t[:].rearrange("p (h x) -> p h x", h=2), in_=w2_v[kind][idx])
-                raw[(kind, idx)] = t
+        def load(kind, idx):
+            if kind == "m":
+                hf, part = divmod(idx, 2)
+                cols = slice(2 * D * part, 2 * D * (part + 1))
+                nc.sync.dma_start(out=mem_sb[hf][:, cols], in_=mem_v[P * hf : P * (hf + 1), cols])
                 return
+            if idx % 2 == 0:
+                big[(kind, idx // 2)] = bigp.tile(
+                    [P, 8192], BF16, tag="big%d" % BIG_SLOT["%s%d" % (kind, idx // 2)], name="raw_%s%d" % (kind, idx // 2)
+                )
+            t = big[(kind, idx // 2)][:, 4096 * (idx % 2) : 4096 * (idx % 2 + 1)]
+            if kind == "k":
+                nc.sync.dma_start(out=t, in_=wk_v[idx])
+            elif kind == "x":
+                nc.sync.dma_start(out=t, in_=x_v[idx])
+            else:
+                nc.sync.dma_start(out=t.rearrange("p (h x) -> p h x", h=2), in_=w2_v[kind][idx])
+            raw[(kind, idx)] = t
 
-        for n in range(RAW_BUFS):
-            advance()
+        w2o = [("e", i) for i in range(4)] + [("a", i) for i in range(4)]
+        for i in range(4):
+            load("k", i)
+        for i in range(4):
+            load("x", i)
+        for i in range(4):
+            if i == MPOS:
+                load("m", 0)
+                load("m", 1)
+            load("e", i)
 
         ident_f = const.tile([P, P], F32)
         masks.make_identity(nc, ident_f[:])
@@ -111,9 +127,9 @@ def tile_ultralightweightmemory_pa_kernel(
         )
         r16 = const.tile([P, 16], BF16)
         nc.vector.tensor_scalar_mul(out=r16[:], in0=r32[:], scalar1=1.0 / 16.0)
-        eps = const.tile([P, 1], F32)
-        nc.vector.memset(eps[:], LN_EPS)
-        nc.scalar.activation(out=warm[:, 0:1], in_=eps[:], func=ACT.Sigmoid)
+        mhalf = const.tile([P, 1], F32)
+        nc.vector.memset(mhalf[:], -0.5)
+        nc.scalar.activation(out=warm[:], in_=mhalf[:], func=ACT.Sigmoid)
 
         def evac(eng, dst, src):
             if eng == "v":
@@ -130,12 +146,20 @@ def tile_ultralightweightmemory_pa_kernel(
             while len(quants) > keep_back:
                 quants.pop(0)()
 
+        tpn = {"n": 0}
+        held = []
+
+        def tp_bank(shape, dtype, name, nb=4):
+            tpn["n"] += 1
+            assert 8 - nb + tpn["n"] % nb not in held
+            return bank(8 - nb + tpn["n"] % nb, shape, dtype, name)
+
         def kunit(j, e):
             rk = raw[("k", j)]
             ce = 2 * j + e
             gk = grpp.tile([P, 2048], BF16, tag="grp", name="gk%d" % ce, align_bytes=64)
             for g in range(4):
-                tp = ps_tp.tile([P, 4, P], BF16, tag="tp", name="tpk%d_%d" % (ce, g))
+                tp = tp_bank([P, 4, P], BF16, "tpk%d_%d" % (ce, g))
                 for t in range(4):
                     d0 = e * D + 512 * g + 128 * t
                     nc.tensor.transpose(tp[:, t, :], rk[:, d0 : d0 + 128], ident_b[:])
@@ -147,247 +171,316 @@ def tile_ultralightweightmemory_pa_kernel(
             quants.append(lambda: quant(ck[:, 512 * ce : 512 * (ce + 1)], sk[:, 512 * ce : 512 * (ce + 1)], gk[:]))
             do_quants(1)
 
-        mean_ps = [ps_acc.tile([P, 4, P], F32, tag="acc", name="mean%d" % g) for g in range(4)]
+        mean_ps = {}
 
         def mean_unit(T):
+            hf, Tl = divmod(T, 4)
+            if Tl == 0:
+                mean_ps[hf] = [bank(z, [P, 8, 64], F32, "mean%d_%d" % (hf, z)) for z in range(2)]
             xt = raw[("x", T)]
             for c in range(16):
                 for i in range(2):
                     nc.tensor.matmul(
-                        mean_ps[c // 4][:, c % 4, 16 * T : 16 * (T + 1)],
+                        mean_ps[hf][c // 8][:, c % 8, 16 * Tl : 16 * (Tl + 1)],
                         lhsT=xt[:, i * D + 128 * c : i * D + 128 * (c + 1)],
                         rhs=r16[:],
                         start=(i == 0),
                         stop=(i == 1),
                     )
 
-        def mean_out():
-            for g in range(4):
-                evac(
-                    "vs"[g % 2],
-                    gm[:, 512 * g : 512 * (g + 1)].rearrange("p (b t) -> p b t", t=4),
-                    mean_ps[g][:].rearrange("p t b -> p b t"),
-                )
-                if g == 2:
-                    quant(cm[:, 0:256], sm[:, 0:256], gm[:, 0:1024])
+        def mean_out(hf):
+            for z in range(2):
+                for g in (z, 2 + z):
+                    src = mean_ps[hf][g // 2][:, 4 * (g % 2) : 4 * (g % 2) + 4, :]
+                    evac(
+                        "vs"[g // 2],
+                        gm[:, 512 * g : 512 * (g + 1)].rearrange("p (b u t) -> p b u t", u=2, t=4),
+                        src.rearrange("p t b -> p b t").unsqueeze(2).to_broadcast([P, 64, 2, 4]),
+                    )
+            quant(cm[:, 0:256], sm[:, 0:256], gm[:, 0:1024])
             quant(cm[:, 256:512], sm[:, 256:512], gm[:, 1024:2048])
 
-        w2 = []
-        for kind, idx in order:
-            if kind in "ea":
-                w2 += [(kind, idx, 0), (kind, idx, 1)]
-        codes = {}
+        pjs = {}
+
+        def stage1(hf, G):
+            pj = bank(2 + 4 * hf + G, [P, 4, P], F32, "pj%d_%d" % (hf, G))
+            pjs[G] = pj
+            for t in range(4):
+                ce = 4 * G + t
+                for g in range(4):
+                    lo = 512 * ce + 128 * g
+                    nc.tensor.matmul_mx(
+                        out=pj[:, t, :],
+                        lhsT=ck[:, lo : lo + 128].bitcast(FP8X4),
+                        lhsT_scale=sk[:, lo : lo + 128],
+                        rhs=cm[:, 128 * g : 128 * (g + 1)].bitcast(FP8X4),
+                        rhs_scale=sm[:, 128 * g : 128 * (g + 1)],
+                        start=(g == 0),
+                        stop=(g == 3),
+                    )
+
+        def proj_quant(G):
+            evac(
+                "v",
+                gp[:, 512 * G : 512 * (G + 1)].rearrange("p (b t) -> p b t", t=4),
+                pjs[G][:].rearrange("p t b -> p b t"),
+            )
+            quant(cp[:, 128 * G : 128 * (G + 1)], sp[:, 128 * G : 128 * (G + 1)], gp[:, 512 * G : 512 * (G + 1)])
+
+        w2 = [(kind, I, h) for kind, I in w2o for h in range(2)]
 
         def prep(idx):
             kind, I, h = w2[idx]
-            rwf = raw[(kind, I)][:].bitcast(F32)
+            rwf = raw[(kind, I)].bitcast(F32)
             gw = grpp.tile([P, 2048], BF16, tag="grp", name="gw%d" % idx, align_bytes=64)
             gwf = gw[:].bitcast(F32)
             for G in range(2):
-                tp = ps_tp.tile([P, 2, 2, P], F32, tag="tp", name="tpw%d_%d" % (idx, G))
+                tp = tp_bank([P, 2, 2, P], F32, "tpw%d_%d" % (idx, G), 2 if idx >= TP2_FROM else 4)
                 for c in range(2):
                     for u in range(2):
                         w0 = (h * 2 + c) * 512 + 256 * G + 128 * u
                         nc.tensor.transpose(tp[:, c, u, :], rwf[:, w0 : w0 + 128], ident_f[:])
                 evac(
-                    EV[(2 * idx + G) % len(EV)],
+                    (EVE if kind == "e" else EVA)[G],
                     gwf[:, 512 * G : 512 * (G + 1)].rearrange("q (p c u) -> q p c u", c=2, u=2),
                     tp[:].rearrange("q c u p -> q p c u"),
                 )
-            if h == 1:
-                advance()
-            if kind == "e":
-                cw = w2cp.tile([P, 512], U32, tag="cw", name="cw%d" % idx, align_bytes=64)
-                sw = w2cp.tile([P, 512], U8, tag="sw", name="sw%d" % idx, align_bytes=64)
-                codes[idx] = (cw[:], sw[:])
-            else:
-                i = 2 * I + h
-                codes[idx] = (ck[:, 512 * i : 512 * (i + 1)], sk[:, 512 * i : 512 * (i + 1)])
-            cwa, swa = codes[idx]
-            quants.append(lambda: quant(cwa, swa, gw[:]))
+            if h == 1 and kind == "e" and I % 2 == 1:
+                load("x", 3 + I)
+                load("x", 4 + I)
+                if I == 3:
+                    load("m", 2)
+                    load("m", 3)
+            i = 2 * I + h
+            quants.append(
+                lambda: quant(cws[kind][:, 512 * i : 512 * (i + 1)], sws[kind][:, 512 * i : 512 * (i + 1)], gw[:])
+            )
 
-        for kind, idx in order:
-            if kind == "x":
-                mean_unit(idx)
-                advance()
-            elif kind == "k":
-                kunit(idx, 0)
-                kunit(idx, 1)
-                advance()
-        do_quants(0)
-        mean_out()
-        for z in range(PRE):
-            prep(z)
-            do_quants(1)
-
-        pj = {}
-
-        def stage1(ce):
-            G, t = divmod(ce, 4)
-            if t == 0:
-                pj[G] = ps_tp.tile([P, 4, P], F32, tag="tp", name="pj%d" % G)
-            for g in range(4):
-                lo = 512 * ce + 128 * g
+        def second(o_ps, kind, I, h):
+            i = 2 * I + h
+            for G in range(2):
+                lo = 512 * i + 256 * G
                 nc.tensor.matmul_mx(
-                    out=pj[G][:, t, :],
-                    lhsT=ck[:, lo : lo + 128].bitcast(FP8X4),
-                    lhsT_scale=sk[:, lo : lo + 128],
-                    rhs=cm[:, 128 * g : 128 * (g + 1)].bitcast(FP8X4),
-                    rhs_scale=sm[:, 128 * g : 128 * (g + 1)],
-                    start=(g == 0),
-                    stop=(g == 3),
-                )
-            if t == 3:
-                evac(
-                    "v",
-                    gp[:, 512 * G : 512 * (G + 1)].rearrange("p (b t) -> p b t", t=4),
-                    pj[G][:].rearrange("p t b -> p b t"),
+                    out=o_ps[:, 256 * h : 256 * (h + 1)],
+                    lhsT=cp[:, 128 * G : 128 * (G + 1)].bitcast(FP8X4),
+                    lhsT_scale=sp[:, 128 * G : 128 * (G + 1)],
+                    rhs=cws[kind][:, lo : lo + 256].bitcast(FP8X4),
+                    rhs_scale=sws[kind][:, lo : lo + 256],
+                    start=(G == 0),
+                    stop=(G == 1),
                 )
 
-        for ce in range(8):
-            stage1(ce)
-            if ce == 5:
-                quant(cp[:, 0:128], sp[:, 0:128], gp[:, 0:512])
-                do_quants(0)
-        quant(cp[:, 128:256], sp[:, 128:256], gp[:, 512:1024])
+        def sigmoid(z_ps, I):
+            nc.scalar.activation(out=g_sb[:, 512 * I : 512 * (I + 1)], in_=z_ps[:], func=ACT.Sigmoid, scale=-1.0)
 
-        def proj(G):
-            return cp[:, 128 * G : 128 * (G + 1)].bitcast(FP8X4), sp[:, 128 * G : 128 * (G + 1)]
+        ybig = {}
 
-        gT = {}
-        gps = {}
+        def yrow(hf, l):
+            return ybig[(hf, l // 2)][:, D * (l % 2) : D * (l % 2 + 1)]
 
-        def zt(I):
-            z = ps_tp.tile([P, 4, P], F32, tag="tp", name="zt%d" % I)
-            for h in range(2):
-                cw, sw = codes[2 * I + h]
-                for j in range(2):
-                    for G in range(2):
-                        lo = 256 * G + 128 * j
-                        pc, ps = proj(G)
-                        nc.tensor.matmul_mx(
-                            out=z[:, 2 * h + j, :],
-                            lhsT=cw[:, lo : lo + 128].bitcast(FP8X4),
-                            lhsT_scale=sw[:, lo : lo + 128],
-                            rhs=pc,
-                            rhs_scale=ps,
-                            start=(G == 0),
-                            stop=(G == 1),
-                        )
-            gT[I] = gtp.tile([P, 512], F32, tag="gT", name="gT%d" % I)
-            nc.scalar.activation(out=gT[I][:], in_=z[:].rearrange("p j b -> p (j b)"), func=ACT.Sigmoid, scale=-1.0)
-            zn = ps_tp.tile([P, 512], F32, tag="tp", name="zn%d" % I)
-            second(zn, 2 * I)
-            nc.scalar.activation(out=g_sb[:, 512 * I : 512 * (I + 1)], in_=zn[:], func=ACT.Sigmoid, scale=-1.0)
-
-        def second(o_ps, idx0):
-            for h in range(2):
-                cw, sw = codes[idx0 + h]
-                for G in range(2):
-                    pc, ps = proj(G)
-                    nc.tensor.matmul_mx(
-                        out=o_ps[:, 256 * h : 256 * (h + 1)],
-                        lhsT=pc,
-                        lhsT_scale=ps,
-                        rhs=cw[:, 256 * G : 256 * (G + 1)].bitcast(FP8X4),
-                        rhs_scale=sw[:, 256 * G : 256 * (G + 1)],
-                        start=(G == 0),
-                        stop=(G == 1),
-                    )
-
-        def gtrans(I):
-            gps[I] = ps_acc.tile([P, 512], F32, tag="acc", name="gps%d" % I)
-            for jj in range(4):
-                nc.tensor.transpose(gps[I][:, 128 * jj : 128 * (jj + 1)], gT[I][:, 128 * jj : 128 * (jj + 1)], ident_f[:])
-
-        n2 = len(w2)
-        for idx in range(PRE, n2 + LAG + GLAG + 1):
-            if idx < n2:
-                prep(idx)
-                do_quants(1)
-            j = idx - LAG
-            if 0 <= j < 8 and j % 2 == 1:
-                zt(j // 2)
-            j = idx - LAG - GLAG
-            if 0 <= j < 8 and j % 2 == 1:
-                gtrans(j // 2)
-        do_quants(0)
-        nc.scalar.activation(out=warm[:, 1:2], in_=g_sb[:, D - 1 : D], func=ACT.Sqrt)
-
-        yv = y[:].rearrange("p (m n) -> p m n", m=M)
-        mv = mem_sb[:].rearrange("p (m n) -> p m n", m=M)
-        vslots = [m for m in range(M) if m not in GSLOTS]
-
-        def gate_v(m0, m1, c):
+        def gate(hf, pr, c):
+            if (hf, pr) not in ybig:
+                ybig[(hf, pr)] = bigp.tile(
+                    [P, 2 * D], F32, tag="big%d" % BIG_SLOT["y%d%d" % (hf, pr)], name="y%d_%d" % (hf, pr)
+                )
             ns = slice(512 * c, 512 * (c + 1))
+            yv = ybig[(hf, pr)][:].rearrange("p (l n) -> p l n", l=2)
+            mv = mem_sb[hf][:].rearrange("p (l n) -> p l n", l=L)
             nc.vector.tensor_tensor(
-                out=yv[:, m0 : m1 + 1, ns],
-                in0=mv[:, m0 : m1 + 1, ns],
-                in1=gps[c][:].unsqueeze(1).to_broadcast([P, m1 - m0 + 1, 512]),
+                out=yv[:, :, ns],
+                in0=mv[:, 2 * pr : 2 * pr + 2, ns],
+                in1=(g_sb[:, ns] if hf == 0 else gps[c][:]).unsqueeze(1).to_broadcast([P, 2, 512]),
                 op=ALU.mult,
             )
 
-        def gate_g(m):
-            nc.gpsimd.tensor_tensor(
-                out=y[:, D * m : D * (m + 1)], in0=mem_sb[:, D * m : D * (m + 1)], in1=g_sb[:], op=ALU.mult
-            )
+        a_ps = {}
 
-        late = [m for i, m in G_LATE]
-        for m in GSLOTS:
-            if m not in late:
-                gate_g(m)
-        for i in range(0, len(vslots), 2):
-            for c in range(4):
-                gate_v(vslots[i], vslots[i + 1], c)
-
-        a_ps = []
-        for I in range(4):
-            a_ps.append(ps_tp.tile([P, 512], F32, tag="tp", name="a%d" % I))
-            second(a_ps[I], 8 + 2 * I)
-
-        def add_slot(m):
-            for I in range(4):
-                ym = y[:, D * m + 512 * I : D * m + 512 * (I + 1)]
+        def add_chunk(hf, I):
+            for l in range(L):
+                ym = yrow(hf, l)[:, 512 * I : 512 * (I + 1)]
                 nc.vector.scalar_tensor_tensor(
                     out=ym,
                     in0=ym,
                     scalar=1.0,
-                    in1=a_ps[I][:],
+                    in1=a_ps[(hf, I)][:],
                     op0=ALU.mult,
                     op1=ALU.add,
-                    accum_out=s4[:, m, I : I + 1],
+                    accum_out=s4[:, L * hf + l, I : I + 1],
+                )
+            if I == 3:
+                nc.vector.tensor_reduce(
+                    out=negs[:, L * hf : L * (hf + 1)],
+                    in_=s4[:, L * hf : L * (hf + 1), :],
+                    axis=mybir.AxisListType.X,
+                    op=ALU.add,
+                    negate=True,
+                )
+
+        def add_slot(hf, l):
+            j = L * hf + l
+            for I in range(4):
+                ym = yrow(hf, l)[:, 512 * I : 512 * (I + 1)]
+                nc.vector.scalar_tensor_tensor(
+                    out=ym,
+                    in0=ym,
+                    scalar=1.0,
+                    in1=a_ps[(hf, I)][:],
+                    op0=ALU.mult,
+                    op1=ALU.add,
+                    accum_out=s4[:, j, I : I + 1],
                 )
             nc.vector.tensor_reduce(
-                out=negs[:, m : m + 1], in_=s4[:, m, :], axis=mybir.AxisListType.X, op=ALU.add, negate=True
+                out=negs[:, j : j + 1], in_=s4[:, j, :], axis=mybir.AxisListType.X, op=ALU.add, negate=True
             )
 
-        border = vslots + GSLOTS
-        add_slot(border[0])
-        for i, m in enumerate(border):
-            if i + 1 < M:
-                add_slot(border[i + 1])
-            ym = y[:, D * m : D * (m + 1)]
-            col = slice(m, m + 1)
+        def finish(hf, l):
+            j = L * hf + l
+            col = slice(j, j + 1)
+            ym = yrow(hf, l)
+            rows = slice(P * hf, P * (hf + 1))
             nc.scalar.activation(
                 out=junk[:], in_=ym, func=ACT.Square, bias=negs[:, col], scale=float(D), accum_out=q[:, col]
             )
-            nc.scalar.activation(out=sd[:, col], in_=q[:, col], func=ACT.Sqrt, bias=eps[:], scale=1.0 / (D * D * D))
             nc.scalar.activation(out=nm[:, col], in_=negs[:, col], func=ACT.Copy, scale=1.0 / D)
-            nc.vector.reciprocal(out=rstd[:, col], in_=sd[:, col])
-            if P4[i] == "v":
-                nt = TAPER if i == M - 1 else 1
-                w = D // nt
-                for z in range(nt):
-                    yz = y[:, D * m + w * z : D * m + w * (z + 1)]
+            nc.gpsimd.tensor_scalar(
+                out=t1[:, col], in0=q[:, col], scalar1=1.0 / (D * D * D), scalar2=LN_EPS, op0=ALU.mult, op1=ALU.add
+            )
+            nc.gpsimd.tensor_tensor(out=rstd[:, col], in0=t1[:, col], in1=mhalf[:], op=ALU.pow)
+            if P4[j] == "v":
+                w = D // TAPER
+                for z in range(TAPER):
+                    yz = ym[:, w * z : w * (z + 1)]
                     nc.vector.tensor_scalar(
                         out=yz, in0=yz, scalar1=nm[:, col], scalar2=rstd[:, col], op0=ALU.add, op1=ALU.mult
                     )
-                    nc.sync.dma_start(out=out_v[:, D * m + w * z : D * m + w * (z + 1)], in_=yz)
+                    nc.sync.dma_start(out=out_v[rows, D * l + w * z : D * l + w * (z + 1)], in_=yz)
             else:
                 nc.gpsimd.tensor_scalar(
                     out=ym, in0=ym, scalar1=nm[:, col], scalar2=rstd[:, col], op0=ALU.add, op1=ALU.mult
                 )
-                nc.sync.dma_start(out=out_v[:, D * m : D * (m + 1)], in_=ym)
-            for ii, mm in G_LATE:
-                if ii == i:
-                    gate_g(mm)
+                nc.sync.dma_start(out=out_v[rows, D * l : D * (l + 1)], in_=ym)
+
+        for j in range(4):
+            kunit(j, 0)
+            kunit(j, 1)
+        for T in range(4):
+            mean_unit(T)
+            if T % 2 == 1:
+                if MPOS == 3 + T:
+                    load("m", 0)
+                    load("m", 1)
+                load("a", T - 1)
+                load("a", T)
+        do_quants(0)
+        mean_out(0)
+        for z in range(PRE):
+            prep(z)
+            do_quants(1)
+        stage1(0, 0)
+        proj_quant(0)
+        do_quants(0)
+        stage1(0, 1)
+        proj_quant(1)
+
+        ready = []
+        o_ps = {}
+
+        def mult(idx):
+            kind, I, h = w2[idx]
+            if h == 0:
+                if kind == "a":
+                    held.append(A_BANK[I])
+                o_ps[(kind, I)] = bank(I % 2 if kind == "e" else A_BANK[I], [P, 512], F32, "o_%s%d" % (kind, I))
+            second(o_ps[(kind, I)], kind, I, h)
+            if h == 1 and kind == "e":
+                sigmoid(o_ps[(kind, I)], I)
+                ready.append(("g", 0, I))
+                ready.append(("g", 1, I))
+            if h == 1 and kind == "a":
+                a_ps[(0, I)] = o_ps[(kind, I)]
+                ready.append(("a", 0, I))
+
+        def filler(idx, budget):
+            if idx < A0_FROM:
+                return
+            for n in range(min(budget, len(ready))):
+                what, pr, c = ready.pop(0)
+                if what == "g":
+                    gate(0, pr, c)
+                else:
+                    add_chunk(0, c)
+
+        done = 0
+        for idx in range(PRE, len(w2) + LAG):
+            if idx < len(w2):
+                prep(idx)
+                do_quants(1)
+            else:
+                do_quants(0)
+            while done <= idx - LAG and done < len(w2):
+                mult(done)
+                done += 1
+            for at, T in MEAN_AT:
+                if at == idx:
+                    mean_unit(T)
+            filler(idx, FILL[idx])
+        mean_unit(7)
+
+        gps = {}
+
+        def zsig(I):
+            assert not [u for u in ready if u[0] == "a" and A_BANK[u[2]] == I]
+            assert len(a_ps) == 4
+            for once in range(1):
+                z_ps = bank(7, [P, 4, P], F32, "zt%d" % I)
+                for jj in range(4):
+                    for G in range(2):
+                        lo = 512 * (2 * I + jj // 2) + 256 * G + 128 * (jj % 2)
+                        nc.tensor.matmul_mx(
+                            out=z_ps[:, jj, :],
+                            lhsT=cws["e"][:, lo : lo + 128].bitcast(FP8X4),
+                            lhsT_scale=sws["e"][:, lo : lo + 128],
+                            rhs=cp[:, 128 * G : 128 * (G + 1)].bitcast(FP8X4),
+                            rhs_scale=sp[:, 128 * G : 128 * (G + 1)],
+                            start=(G == 0),
+                            stop=(G == 1),
+                        )
+                nc.scalar.activation(
+                    out=g_sb[:, 512 * I : 512 * (I + 1)],
+                    in_=z_ps[:].rearrange("p j b -> p (j b)"),
+                    func=ACT.Sigmoid,
+                    scale=-1.0,
+                )
+                gps[I] = bank(I, [P, 512], F32, "gps%d" % I)
+                for jj in range(4):
+                    lo = 512 * I + 128 * jj
+                    nc.tensor.transpose(gps[I][:, 128 * jj : 128 * (jj + 1)], g_sb[:, lo : lo + 128], ident_f[:])
+
+        def amm():
+            for I in range(4):
+                a_ps[(1, I)] = bank(4 + I, [P, 512], F32, "a1_%d" % I)
+                second(a_ps[(1, I)], "a", I, 0)
+                second(a_ps[(1, I)], "a", I, 1)
+
+        for step in SEQ0:
+            if step[0] == "u":
+                filler(99, int(step[1]))
+            elif step[0] == "f":
+                finish(0, int(step[1]))
+            elif step == "M":
+                mean_out(1)
+                stage1(1, 0)
+                stage1(1, 1)
+            elif step[0] == "p":
+                proj_quant(int(step[1]))
+            elif step[0] == "z":
+                zsig(int(step[1]))
+        amm()
+        for I in range(4):
+            gate(1, 0, I)
+            gate(1, 1, I)
+        add_slot(1, 0)
+        for l in range(L):
+            if l + 1 < L:
+                add_slot(1, l + 1)
+            finish(1, l)

@@ -15,25 +15,21 @@ ACT = mybir.ActivationFunctionType
 
 P = 128
 D = 2048
-R = 1024
-L = 4
+ROWS = 4
+CHUNK = 512
 LN_EPS = 1e-5
+STEPS = 16
+LAST_PIECES = 4
 
-BIG_SLOT = {"k0": 0, "k1": 1, "x0": 2, "x1": 3, "e0": 4, "e1": 5, "a0": 2, "a1": 3, "x2": 4, "x3": 5, "y00": 0, "y01": 1, "y10": 2, "y11": 3}
-MEAN_AT = [(13, 4),(15, 5),(16, 6)]
-TP2_FROM = 15
-A_BANK = [2, 3, 4, 5]
-GRP_BUFS = 4
-EVE = "ss"
-EVA = "ss"
-A0_FROM = 4
-PRE = 3
-LAG = 2
-FILL = [0,0,1,0,1,1,1,0,1,1,1,1,1,0,1,0,0,0,0]
-MPOS = 4
-SEQ0 = ["u1","M","u1","p0","p1","u9","z0","z1","f0","z2","f1","z3","f2","f3"]
-P4 = "ggggggvv"
-TAPER = 4
+SLOT_OF = {
+    "k0": 0, "y00": 0,
+    "k1": 1, "y01": 1,
+    "x0": 2, "a0": 2, "y10": 2,
+    "x1": 3, "a1": 3, "y11": 3,
+    "e0": 4, "x2": 4,
+    "e1": 5, "x3": 5,
+}
+ADD_BANK = [2, 3, 4, 5]
 
 
 def tile_ultralightweightmemory_pa_kernel(
@@ -43,8 +39,8 @@ def tile_ultralightweightmemory_pa_kernel(
     with ExitStack() as ctx:
         const = ctx.enter_context(tc.tile_pool(name="const", bufs=1))
         keep = ctx.enter_context(tc.tile_pool(name="keep", bufs=1))
-        bigp = ctx.enter_context(tc.tile_pool(name="bigp", bufs=1))
-        grpp = ctx.enter_context(tc.tile_pool(name="grpp", bufs=GRP_BUFS))
+        slots = ctx.enter_context(tc.tile_pool(name="slots", bufs=1))
+        grouped = ctx.enter_context(tc.tile_pool(name="grouped", bufs=4))
         psum = ctx.enter_context(tc.psum_pool(name="psum", bufs=1))
         ctx.enter_context(tc.manual_schedule())
 
@@ -60,44 +56,42 @@ def tile_ultralightweightmemory_pa_kernel(
         mem_v = memory.rearrange("b (u l) n -> (b u) (l n)", u=2)
         out_v = out.rearrange("b (u l) n -> (b u) (l n)", u=2)
 
-        mem_sb = [keep.tile([P, L * D], BF16, name="mem%d" % hf) for hf in range(2)]
-        g_sb = keep.tile([P, D], F32)
-        junk = keep.tile([P, D], BF16)
-        cws = {}
-        sws = {}
+        mem_sb = [keep.tile([P, ROWS * D], BF16, name="mem%d" % half) for half in range(2)]
+        gate_sb = keep.tile([P, D], F32)
+        squares = keep.tile([P, D], BF16)
+        words = {}
+        scales = {}
         for kind in "kea":
-            cws[kind] = keep.tile([P, 4096], U32, name="c_%s" % kind, align_bytes=64)
-            sws[kind] = keep.tile([P, 4096], U8, name="s_%s" % kind, align_bytes=64)
-        ck = cws["k"]
-        sk = sws["k"]
-        gm = keep.tile([P, 2048], BF16, align_bytes=64)
-        cm = keep.tile([P, 512], U32, align_bytes=64)
-        sm = keep.tile([P, 512], U8, align_bytes=64)
-        gp = keep.tile([P, 1024], BF16, align_bytes=64)
-        cp = keep.tile([P, 256], U32, align_bytes=64)
-        sp = keep.tile([P, 256], U8, align_bytes=64)
-        s4 = keep.tile([P, 2 * L, 4], F32)
-        negs = keep.tile([P, 2 * L], F32)
-        nm = keep.tile([P, 2 * L], F32)
-        q = keep.tile([P, 2 * L], F32)
-        t1 = keep.tile([P, 2 * L], F32)
-        rstd = keep.tile([P, 2 * L], F32)
-        warm = keep.tile([P, 1], F32)
+            words[kind] = keep.tile([P, 4096], U32, name="words_%s" % kind, align_bytes=64)
+            scales[kind] = keep.tile([P, 4096], U8, name="scales_%s" % kind, align_bytes=64)
+        mean_bf = keep.tile([P, 2048], BF16, align_bytes=64)
+        mean_words = keep.tile([P, 512], U32, align_bytes=64)
+        mean_scales = keep.tile([P, 512], U8, align_bytes=64)
+        proj_bf = keep.tile([P, 1024], BF16, align_bytes=64)
+        proj_words = keep.tile([P, 256], U32, align_bytes=64)
+        proj_scales = keep.tile([P, 256], U8, align_bytes=64)
+        part_sums = keep.tile([P, 2 * ROWS, 4], F32)
+        neg_sum = keep.tile([P, 2 * ROWS], F32)
+        neg_mean = keep.tile([P, 2 * ROWS], F32)
+        sq_sum = keep.tile([P, 2 * ROWS], F32)
+        var_eps = keep.tile([P, 2 * ROWS], F32)
+        rstd = keep.tile([P, 2 * ROWS], F32)
+        table_warm = keep.tile([P, 1], F32)
 
         raw = {}
-        big = {}
+        slot_tile = {}
 
         def load(kind, idx):
             if kind == "m":
-                hf, part = divmod(idx, 2)
+                half, part = divmod(idx, 2)
                 cols = slice(2 * D * part, 2 * D * (part + 1))
-                nc.sync.dma_start(out=mem_sb[hf][:, cols], in_=mem_v[P * hf : P * (hf + 1), cols])
+                nc.sync.dma_start(out=mem_sb[half][:, cols], in_=mem_v[P * half : P * (half + 1), cols])
                 return
             if idx % 2 == 0:
-                big[(kind, idx // 2)] = bigp.tile(
-                    [P, 8192], BF16, tag="big%d" % BIG_SLOT["%s%d" % (kind, idx // 2)], name="raw_%s%d" % (kind, idx // 2)
+                slot_tile[(kind, idx // 2)] = slots.tile(
+                    [P, 8192], BF16, tag="slot%d" % SLOT_OF["%s%d" % (kind, idx // 2)], name="raw_%s%d" % (kind, idx // 2)
                 )
-            t = big[(kind, idx // 2)][:, 4096 * (idx % 2) : 4096 * (idx % 2 + 1)]
+            t = slot_tile[(kind, idx // 2)][:, 4096 * (idx % 2) : 4096 * (idx % 2 + 1)]
             if kind == "k":
                 nc.sync.dma_start(out=t, in_=wk_v[idx])
             elif kind == "x":
@@ -106,381 +100,350 @@ def tile_ultralightweightmemory_pa_kernel(
                 nc.sync.dma_start(out=t.rearrange("p (h x) -> p h x", h=2), in_=w2_v[kind][idx])
             raw[(kind, idx)] = t
 
-        w2o = [("e", i) for i in range(4)] + [("a", i) for i in range(4)]
         for i in range(4):
             load("k", i)
         for i in range(4):
             load("x", i)
         for i in range(4):
-            if i == MPOS:
-                load("m", 0)
-                load("m", 1)
             load("e", i)
 
         ident_f = const.tile([P, P], F32)
         masks.make_identity(nc, ident_f[:])
         ident_b = const.tile([P, P], BF16)
         masks.make_identity(nc, ident_b[:])
-        r32 = const.tile([P, 16], F32)
+        member = const.tile([P, 16], F32)
         nc.vector.tensor_reduce(
-            out=r32[:], in_=ident_f[:].rearrange("p (n s) -> p n s", s=8), axis=mybir.AxisListType.X, op=ALU.add
+            out=member[:], in_=ident_f[:].rearrange("p (n s) -> p n s", s=8), axis=mybir.AxisListType.X, op=ALU.add
         )
-        r16 = const.tile([P, 16], BF16)
-        nc.vector.tensor_scalar_mul(out=r16[:], in0=r32[:], scalar1=1.0 / 16.0)
-        mhalf = const.tile([P, 1], F32)
-        nc.vector.memset(mhalf[:], -0.5)
-        nc.scalar.activation(out=warm[:], in_=mhalf[:], func=ACT.Sigmoid)
+        averager = const.tile([P, 16], BF16)
+        nc.vector.tensor_scalar_mul(out=averager[:], in0=member[:], scalar1=1.0 / 16.0)
+        minus_half = const.tile([P, 1], F32)
+        nc.vector.memset(minus_half[:], -0.5)
+        nc.scalar.activation(out=table_warm[:], in_=minus_half[:], func=ACT.Sigmoid)
 
-        def evac(eng, dst, src):
-            if eng == "v":
+        def copy_out(engine, dst, src):
+            if engine == "v":
                 nc.vector.tensor_copy(out=dst, in_=src)
             else:
                 nc.scalar.copy(out=dst, in_=src)
 
-        def quant(codes_ap, scales_ap, in_ap):
-            nc.vector.quantize_mx(out=codes_ap.bitcast(FP8X4), scales=scales_ap, in_=in_ap)
+        def quantise(words_ap, scales_ap, in_ap):
+            nc.vector.quantize_mx(out=words_ap.bitcast(FP8X4), scales=scales_ap, in_=in_ap)
 
-        quants = []
+        waiting = []
 
-        def do_quants(keep_back):
-            while len(quants) > keep_back:
-                quants.pop(0)()
+        def quantise_waiting(keep_back):
+            while len(waiting) > keep_back:
+                waiting.pop(0)()
 
-        tpn = {"n": 0}
-        held = []
+        turn = {"n": 0}
 
-        def tp_bank(shape, dtype, name, nb=4):
-            tpn["n"] += 1
-            assert 8 - nb + tpn["n"] % nb not in held
-            return bank(8 - nb + tpn["n"] % nb, shape, dtype, name)
+        def transpose_bank(shape, dtype, name, banks=4):
+            turn["n"] += 1
+            return bank(8 - banks + turn["n"] % banks, shape, dtype, name)
 
-        def kunit(j, e):
-            rk = raw[("k", j)]
+        def prepare_key(j, e):
+            loaded = raw[("k", j)]
             ce = 2 * j + e
-            gk = grpp.tile([P, 2048], BF16, tag="grp", name="gk%d" % ce, align_bytes=64)
+            group = grouped.tile([P, 2048], BF16, tag="grp", name="gk%d" % ce, align_bytes=64)
             for g in range(4):
-                tp = tp_bank([P, 4, P], BF16, "tpk%d_%d" % (ce, g))
+                tp = transpose_bank([P, 4, P], BF16, "tpk%d_%d" % (ce, g))
                 for t in range(4):
                     d0 = e * D + 512 * g + 128 * t
-                    nc.tensor.transpose(tp[:, t, :], rk[:, d0 : d0 + 128], ident_b[:])
-                evac(
+                    nc.tensor.transpose(tp[:, t, :], loaded[:, d0 : d0 + 128], ident_b[:])
+                copy_out(
                     "vs"[g % 2],
-                    gk[:, 512 * g : 512 * (g + 1)].rearrange("p (c t) -> p c t", t=4),
+                    group[:, 512 * g : 512 * (g + 1)].rearrange("p (c t) -> p c t", t=4),
                     tp[:].rearrange("p t c -> p c t"),
                 )
-            quants.append(lambda: quant(ck[:, 512 * ce : 512 * (ce + 1)], sk[:, 512 * ce : 512 * (ce + 1)], gk[:]))
-            do_quants(1)
+            cols = slice(512 * ce, 512 * (ce + 1))
+            waiting.append(lambda: quantise(words["k"][:, cols], scales["k"][:, cols], group[:]))
+            quantise_waiting(1)
 
         mean_ps = {}
 
-        def mean_unit(T):
-            hf, Tl = divmod(T, 4)
+        def mean_chunk(T):
+            half, Tl = divmod(T, 4)
             if Tl == 0:
-                mean_ps[hf] = [bank(z, [P, 8, 64], F32, "mean%d_%d" % (hf, z)) for z in range(2)]
+                mean_ps[half] = [bank(z, [P, 8, 64], F32, "mean%d_%d" % (half, z)) for z in range(2)]
             xt = raw[("x", T)]
             for c in range(16):
                 for i in range(2):
                     nc.tensor.matmul(
-                        mean_ps[hf][c // 8][:, c % 8, 16 * Tl : 16 * (Tl + 1)],
+                        mean_ps[half][c // 8][:, c % 8, 16 * Tl : 16 * (Tl + 1)],
                         lhsT=xt[:, i * D + 128 * c : i * D + 128 * (c + 1)],
-                        rhs=r16[:],
+                        rhs=averager[:],
                         start=(i == 0),
                         stop=(i == 1),
                     )
 
-        def mean_out(hf):
+        def mean_out(half):
             for z in range(2):
                 for g in (z, 2 + z):
-                    src = mean_ps[hf][g // 2][:, 4 * (g % 2) : 4 * (g % 2) + 4, :]
-                    evac(
+                    src = mean_ps[half][g // 2][:, 4 * (g % 2) : 4 * (g % 2) + 4, :]
+                    copy_out(
                         "vs"[g // 2],
-                        gm[:, 512 * g : 512 * (g + 1)].rearrange("p (b u t) -> p b u t", u=2, t=4),
+                        mean_bf[:, 512 * g : 512 * (g + 1)].rearrange("p (b u t) -> p b u t", u=2, t=4),
                         src.rearrange("p t b -> p b t").unsqueeze(2).to_broadcast([P, 64, 2, 4]),
                     )
-            quant(cm[:, 0:256], sm[:, 0:256], gm[:, 0:1024])
-            quant(cm[:, 256:512], sm[:, 256:512], gm[:, 1024:2048])
+            quantise(mean_words[:, 0:256], mean_scales[:, 0:256], mean_bf[:, 0:1024])
+            quantise(mean_words[:, 256:512], mean_scales[:, 256:512], mean_bf[:, 1024:2048])
 
-        pjs = {}
+        proj_ps = {}
 
-        def stage1(hf, G):
-            pj = bank(2 + 4 * hf + G, [P, 4, P], F32, "pj%d_%d" % (hf, G))
-            pjs[G] = pj
+        def first_matmul(half, G):
+            pj = bank(2 + 4 * half + G, [P, 4, P], F32, "pj%d_%d" % (half, G))
+            proj_ps[G] = pj
             for t in range(4):
                 ce = 4 * G + t
                 for g in range(4):
                     lo = 512 * ce + 128 * g
                     nc.tensor.matmul_mx(
                         out=pj[:, t, :],
-                        lhsT=ck[:, lo : lo + 128].bitcast(FP8X4),
-                        lhsT_scale=sk[:, lo : lo + 128],
-                        rhs=cm[:, 128 * g : 128 * (g + 1)].bitcast(FP8X4),
-                        rhs_scale=sm[:, 128 * g : 128 * (g + 1)],
+                        lhsT=words["k"][:, lo : lo + 128].bitcast(FP8X4),
+                        lhsT_scale=scales["k"][:, lo : lo + 128],
+                        rhs=mean_words[:, 128 * g : 128 * (g + 1)].bitcast(FP8X4),
+                        rhs_scale=mean_scales[:, 128 * g : 128 * (g + 1)],
                         start=(g == 0),
                         stop=(g == 3),
                     )
 
-        def proj_quant(G):
-            evac(
+        def proj_out(G):
+            copy_out(
                 "v",
-                gp[:, 512 * G : 512 * (G + 1)].rearrange("p (b t) -> p b t", t=4),
-                pjs[G][:].rearrange("p t b -> p b t"),
+                proj_bf[:, 512 * G : 512 * (G + 1)].rearrange("p (b t) -> p b t", t=4),
+                proj_ps[G][:].rearrange("p t b -> p b t"),
             )
-            quant(cp[:, 128 * G : 128 * (G + 1)], sp[:, 128 * G : 128 * (G + 1)], gp[:, 512 * G : 512 * (G + 1)])
+            cols = slice(128 * G, 128 * (G + 1))
+            quantise(proj_words[:, cols], proj_scales[:, cols], proj_bf[:, 512 * G : 512 * (G + 1)])
 
-        w2 = [(kind, I, h) for kind, I in w2o for h in range(2)]
+        chunks = [("e", I) for I in range(4)] + [("a", I) for I in range(4)]
 
-        def prep(idx):
-            kind, I, h = w2[idx]
-            rwf = raw[(kind, I)].bitcast(F32)
-            gw = grpp.tile([P, 2048], BF16, tag="grp", name="gw%d" % idx, align_bytes=64)
-            gwf = gw[:].bitcast(F32)
+        def prepare(step):
+            kind, I = chunks[step // 2]
+            h = step % 2
+            r_pairs = raw[(kind, I)].bitcast(F32)
+            group = grouped.tile([P, 2048], BF16, tag="grp", name="gw%d" % step, align_bytes=64)
+            group_r_pairs = group[:].bitcast(F32)
             for G in range(2):
-                tp = tp_bank([P, 2, 2, P], F32, "tpw%d_%d" % (idx, G), 2 if idx >= TP2_FROM else 4)
+                tp = transpose_bank([P, 2, 2, P], F32, "tpw%d_%d" % (step, G), 2 if step >= STEPS - 2 else 4)
                 for c in range(2):
                     for u in range(2):
                         w0 = (h * 2 + c) * 512 + 256 * G + 128 * u
-                        nc.tensor.transpose(tp[:, c, u, :], rwf[:, w0 : w0 + 128], ident_f[:])
-                evac(
-                    (EVE if kind == "e" else EVA)[G],
-                    gwf[:, 512 * G : 512 * (G + 1)].rearrange("q (p c u) -> q p c u", c=2, u=2),
+                        nc.tensor.transpose(tp[:, c, u, :], r_pairs[:, w0 : w0 + 128], ident_f[:])
+                copy_out(
+                    "s",
+                    group_r_pairs[:, 512 * G : 512 * (G + 1)].rearrange("q (p c u) -> q p c u", c=2, u=2),
                     tp[:].rearrange("q c u p -> q p c u"),
                 )
-            if h == 1 and kind == "e" and I % 2 == 1:
+            if kind == "e" and step % 4 == 3:
                 load("x", 3 + I)
                 load("x", 4 + I)
                 if I == 3:
                     load("m", 2)
                     load("m", 3)
-            i = 2 * I + h
-            quants.append(
-                lambda: quant(cws[kind][:, 512 * i : 512 * (i + 1)], sws[kind][:, 512 * i : 512 * (i + 1)], gw[:])
+            cols = slice(512 * (2 * I + h), 512 * (2 * I + h + 1))
+            waiting.append(lambda: quantise(words[kind][:, cols], scales[kind][:, cols], group[:]))
+
+        def second_matmul(o_ps, kind, I):
+            for h in range(2):
+                for G in range(2):
+                    lo = 512 * (2 * I + h) + 256 * G
+                    nc.tensor.matmul_mx(
+                        out=o_ps[:, 256 * h : 256 * (h + 1)],
+                        lhsT=proj_words[:, 128 * G : 128 * (G + 1)].bitcast(FP8X4),
+                        lhsT_scale=proj_scales[:, 128 * G : 128 * (G + 1)],
+                        rhs=words[kind][:, lo : lo + 256].bitcast(FP8X4),
+                        rhs_scale=scales[kind][:, lo : lo + 256],
+                        start=(G == 0),
+                        stop=(G == 1),
+                    )
+
+        add_ps = {}
+        gate_ps = {}
+
+        def first_half_products(kind, I):
+            if kind == "e":
+                o_ps = bank(I % 2, [P, CHUNK], F32, "o_e%d" % I)
+                second_matmul(o_ps, kind, I)
+                nc.scalar.activation(
+                    out=gate_sb[:, CHUNK * I : CHUNK * (I + 1)], in_=o_ps[:], func=ACT.Sigmoid, scale=-1.0
+                )
+            else:
+                add_ps[(0, I)] = bank(ADD_BANK[I], [P, CHUNK], F32, "o_a%d" % I)
+                second_matmul(add_ps[(0, I)], kind, I)
+
+        def second_half_gate(I):
+            z_ps = bank(7, [P, 4, P], F32, "zt%d" % I)
+            for jj in range(4):
+                for G in range(2):
+                    lo = 512 * (2 * I + jj // 2) + 256 * G + 128 * (jj % 2)
+                    nc.tensor.matmul_mx(
+                        out=z_ps[:, jj, :],
+                        lhsT=words["e"][:, lo : lo + 128].bitcast(FP8X4),
+                        lhsT_scale=scales["e"][:, lo : lo + 128],
+                        rhs=proj_words[:, 128 * G : 128 * (G + 1)].bitcast(FP8X4),
+                        rhs_scale=proj_scales[:, 128 * G : 128 * (G + 1)],
+                        start=(G == 0),
+                        stop=(G == 1),
+                    )
+            nc.scalar.activation(
+                out=gate_sb[:, CHUNK * I : CHUNK * (I + 1)],
+                in_=z_ps[:].rearrange("p j b -> p (j b)"),
+                func=ACT.Sigmoid,
+                scale=-1.0,
             )
+            gate_ps[I] = bank(I, [P, CHUNK], F32, "gps%d" % I)
+            for jj in range(4):
+                lo = CHUNK * I + 128 * jj
+                nc.tensor.transpose(gate_ps[I][:, 128 * jj : 128 * (jj + 1)], gate_sb[:, lo : lo + 128], ident_f[:])
 
-        def second(o_ps, kind, I, h):
-            i = 2 * I + h
-            for G in range(2):
-                lo = 512 * i + 256 * G
-                nc.tensor.matmul_mx(
-                    out=o_ps[:, 256 * h : 256 * (h + 1)],
-                    lhsT=cp[:, 128 * G : 128 * (G + 1)].bitcast(FP8X4),
-                    lhsT_scale=sp[:, 128 * G : 128 * (G + 1)],
-                    rhs=cws[kind][:, lo : lo + 256].bitcast(FP8X4),
-                    rhs_scale=sws[kind][:, lo : lo + 256],
-                    start=(G == 0),
-                    stop=(G == 1),
+        y_tile = {}
+
+        def y_row(half, l):
+            return y_tile[(half, l // 2)][:, D * (l % 2) : D * (l % 2 + 1)]
+
+        def multiply(half, k, I):
+            if (half, k) not in y_tile:
+                y_tile[(half, k)] = slots.tile(
+                    [P, 2 * D], F32, tag="slot%d" % SLOT_OF["y%d%d" % (half, k)], name="y%d_%d" % (half, k)
                 )
-
-        def sigmoid(z_ps, I):
-            nc.scalar.activation(out=g_sb[:, 512 * I : 512 * (I + 1)], in_=z_ps[:], func=ACT.Sigmoid, scale=-1.0)
-
-        ybig = {}
-
-        def yrow(hf, l):
-            return ybig[(hf, l // 2)][:, D * (l % 2) : D * (l % 2 + 1)]
-
-        def gate(hf, pr, c):
-            if (hf, pr) not in ybig:
-                ybig[(hf, pr)] = bigp.tile(
-                    [P, 2 * D], F32, tag="big%d" % BIG_SLOT["y%d%d" % (hf, pr)], name="y%d_%d" % (hf, pr)
-                )
-            ns = slice(512 * c, 512 * (c + 1))
-            yv = ybig[(hf, pr)][:].rearrange("p (l n) -> p l n", l=2)
-            mv = mem_sb[hf][:].rearrange("p (l n) -> p l n", l=L)
+            ns = slice(CHUNK * I, CHUNK * (I + 1))
+            yv = y_tile[(half, k)][:].rearrange("p (l n) -> p l n", l=2)
+            mv = mem_sb[half][:].rearrange("p (l n) -> p l n", l=ROWS)
             nc.vector.tensor_tensor(
                 out=yv[:, :, ns],
-                in0=mv[:, 2 * pr : 2 * pr + 2, ns],
-                in1=(g_sb[:, ns] if hf == 0 else gps[c][:]).unsqueeze(1).to_broadcast([P, 2, 512]),
+                in0=mv[:, 2 * k : 2 * k + 2, ns],
+                in1=(gate_sb[:, ns] if half == 0 else gate_ps[I][:]).unsqueeze(1).to_broadcast([P, 2, CHUNK]),
                 op=ALU.mult,
             )
 
-        a_ps = {}
+        def add(half, l, I):
+            ym = y_row(half, l)[:, CHUNK * I : CHUNK * (I + 1)]
+            nc.vector.scalar_tensor_tensor(
+                out=ym,
+                in0=ym,
+                scalar=1.0,
+                in1=add_ps[(half, I)][:],
+                op0=ALU.mult,
+                op1=ALU.add,
+                accum_out=part_sums[:, ROWS * half + l, I : I + 1],
+            )
 
-        def add_chunk(hf, I):
-            for l in range(L):
-                ym = yrow(hf, l)[:, 512 * I : 512 * (I + 1)]
-                nc.vector.scalar_tensor_tensor(
-                    out=ym,
-                    in0=ym,
-                    scalar=1.0,
-                    in1=a_ps[(hf, I)][:],
-                    op0=ALU.mult,
-                    op1=ALU.add,
-                    accum_out=s4[:, L * hf + l, I : I + 1],
-                )
-            if I == 3:
-                nc.vector.tensor_reduce(
-                    out=negs[:, L * hf : L * (hf + 1)],
-                    in_=s4[:, L * hf : L * (hf + 1), :],
-                    axis=mybir.AxisListType.X,
-                    op=ALU.add,
-                    negate=True,
-                )
-
-        def add_slot(hf, l):
-            j = L * hf + l
-            for I in range(4):
-                ym = yrow(hf, l)[:, 512 * I : 512 * (I + 1)]
-                nc.vector.scalar_tensor_tensor(
-                    out=ym,
-                    in0=ym,
-                    scalar=1.0,
-                    in1=a_ps[(hf, I)][:],
-                    op0=ALU.mult,
-                    op1=ALU.add,
-                    accum_out=s4[:, j, I : I + 1],
-                )
+        def total(first, count):
             nc.vector.tensor_reduce(
-                out=negs[:, j : j + 1], in_=s4[:, j, :], axis=mybir.AxisListType.X, op=ALU.add, negate=True
+                out=neg_sum[:, first : first + count],
+                in_=part_sums[:, first : first + count, :],
+                axis=mybir.AxisListType.X,
+                op=ALU.add,
+                negate=True,
             )
 
-        def finish(hf, l):
-            j = L * hf + l
+        def add_chunk(I):
+            for l in range(ROWS):
+                add(0, l, I)
+            if I == 3:
+                total(0, ROWS)
+
+        def add_row(l):
+            for I in range(4):
+                add(1, l, I)
+            total(ROWS + l, 1)
+
+        def finish(half, l):
+            j = ROWS * half + l
             col = slice(j, j + 1)
-            ym = yrow(hf, l)
-            rows = slice(P * hf, P * (hf + 1))
+            ym = y_row(half, l)
+            hbm_rows = slice(P * half, P * (half + 1))
             nc.scalar.activation(
-                out=junk[:], in_=ym, func=ACT.Square, bias=negs[:, col], scale=float(D), accum_out=q[:, col]
+                out=squares[:], in_=ym, func=ACT.Square, bias=neg_sum[:, col], scale=float(D), accum_out=sq_sum[:, col]
             )
-            nc.scalar.activation(out=nm[:, col], in_=negs[:, col], func=ACT.Copy, scale=1.0 / D)
+            nc.scalar.activation(out=neg_mean[:, col], in_=neg_sum[:, col], func=ACT.Copy, scale=1.0 / D)
             nc.gpsimd.tensor_scalar(
-                out=t1[:, col], in0=q[:, col], scalar1=1.0 / (D * D * D), scalar2=LN_EPS, op0=ALU.mult, op1=ALU.add
+                out=var_eps[:, col],
+                in0=sq_sum[:, col],
+                scalar1=1.0 / (D * D * D),
+                scalar2=LN_EPS,
+                op0=ALU.mult,
+                op1=ALU.add,
             )
-            nc.gpsimd.tensor_tensor(out=rstd[:, col], in0=t1[:, col], in1=mhalf[:], op=ALU.pow)
-            if P4[j] == "v":
-                w = D // TAPER
-                for z in range(TAPER):
+            nc.gpsimd.tensor_tensor(out=rstd[:, col], in0=var_eps[:, col], in1=minus_half[:], op=ALU.pow)
+            if j >= 2 * ROWS - 2:
+                w = D // LAST_PIECES
+                for z in range(LAST_PIECES):
                     yz = ym[:, w * z : w * (z + 1)]
                     nc.vector.tensor_scalar(
-                        out=yz, in0=yz, scalar1=nm[:, col], scalar2=rstd[:, col], op0=ALU.add, op1=ALU.mult
+                        out=yz, in0=yz, scalar1=neg_mean[:, col], scalar2=rstd[:, col], op0=ALU.add, op1=ALU.mult
                     )
-                    nc.sync.dma_start(out=out_v[rows, D * l + w * z : D * l + w * (z + 1)], in_=yz)
+                    nc.sync.dma_start(out=out_v[hbm_rows, D * l + w * z : D * l + w * (z + 1)], in_=yz)
             else:
                 nc.gpsimd.tensor_scalar(
-                    out=ym, in0=ym, scalar1=nm[:, col], scalar2=rstd[:, col], op0=ALU.add, op1=ALU.mult
+                    out=ym, in0=ym, scalar1=neg_mean[:, col], scalar2=rstd[:, col], op0=ALU.add, op1=ALU.mult
                 )
-                nc.sync.dma_start(out=out_v[rows, D * l : D * (l + 1)], in_=ym)
+                nc.sync.dma_start(out=out_v[hbm_rows, D * l : D * (l + 1)], in_=ym)
 
         for j in range(4):
-            kunit(j, 0)
-            kunit(j, 1)
+            prepare_key(j, 0)
+            prepare_key(j, 1)
         for T in range(4):
-            mean_unit(T)
+            mean_chunk(T)
             if T % 2 == 1:
-                if MPOS == 3 + T:
+                if T == 1:
                     load("m", 0)
                     load("m", 1)
                 load("a", T - 1)
                 load("a", T)
-        do_quants(0)
+        quantise_waiting(0)
         mean_out(0)
-        for z in range(PRE):
-            prep(z)
-            do_quants(1)
-        stage1(0, 0)
-        proj_quant(0)
-        do_quants(0)
-        stage1(0, 1)
-        proj_quant(1)
+        for step in range(2):
+            prepare(step)
+            quantise_waiting(1)
+        first_matmul(0, 0)
+        proj_out(0)
+        quantise_waiting(0)
+        first_matmul(0, 1)
+        proj_out(1)
 
-        ready = []
-        o_ps = {}
-
-        def mult(idx):
-            kind, I, h = w2[idx]
-            if h == 0:
-                if kind == "a":
-                    held.append(A_BANK[I])
-                o_ps[(kind, I)] = bank(I % 2 if kind == "e" else A_BANK[I], [P, 512], F32, "o_%s%d" % (kind, I))
-            second(o_ps[(kind, I)], kind, I, h)
-            if h == 1 and kind == "e":
-                sigmoid(o_ps[(kind, I)], I)
-                ready.append(("g", 0, I))
-                ready.append(("g", 1, I))
-            if h == 1 and kind == "a":
-                a_ps[(0, I)] = o_ps[(kind, I)]
-                ready.append(("a", 0, I))
-
-        def filler(idx, budget):
-            if idx < A0_FROM:
-                return
-            for n in range(min(budget, len(ready))):
-                what, pr, c = ready.pop(0)
-                if what == "g":
-                    gate(0, pr, c)
-                else:
-                    add_chunk(0, c)
-
-        done = 0
-        for idx in range(PRE, len(w2) + LAG):
-            if idx < len(w2):
-                prep(idx)
-                do_quants(1)
+        for step in range(2, STEPS + 2):
+            if step < STEPS:
+                prepare(step)
+                quantise_waiting(1)
             else:
-                do_quants(0)
-            while done <= idx - LAG and done < len(w2):
-                mult(done)
-                done += 1
-            for at, T in MEAN_AT:
-                if at == idx:
-                    mean_unit(T)
-            filler(idx, FILL[idx])
-        mean_unit(7)
+                quantise_waiting(0)
+            if step % 2 == 1:
+                kind, I = chunks[(step - 3) // 2]
+                first_half_products(kind, I)
+            if step >= STEPS - 2:
+                mean_chunk(step - STEPS + 6)
+            if 4 <= step < 12:
+                multiply(0, step % 2, (step - 4) // 2)
+            if step == 12:
+                add_chunk(0)
 
-        gps = {}
-
-        def zsig(I):
-            assert not [u for u in ready if u[0] == "a" and A_BANK[u[2]] == I]
-            assert len(a_ps) == 4
-            for once in range(1):
-                z_ps = bank(7, [P, 4, P], F32, "zt%d" % I)
-                for jj in range(4):
-                    for G in range(2):
-                        lo = 512 * (2 * I + jj // 2) + 256 * G + 128 * (jj % 2)
-                        nc.tensor.matmul_mx(
-                            out=z_ps[:, jj, :],
-                            lhsT=cws["e"][:, lo : lo + 128].bitcast(FP8X4),
-                            lhsT_scale=sws["e"][:, lo : lo + 128],
-                            rhs=cp[:, 128 * G : 128 * (G + 1)].bitcast(FP8X4),
-                            rhs_scale=sp[:, 128 * G : 128 * (G + 1)],
-                            start=(G == 0),
-                            stop=(G == 1),
-                        )
-                nc.scalar.activation(
-                    out=g_sb[:, 512 * I : 512 * (I + 1)],
-                    in_=z_ps[:].rearrange("p j b -> p (j b)"),
-                    func=ACT.Sigmoid,
-                    scale=-1.0,
-                )
-                gps[I] = bank(I, [P, 512], F32, "gps%d" % I)
-                for jj in range(4):
-                    lo = 512 * I + 128 * jj
-                    nc.tensor.transpose(gps[I][:, 128 * jj : 128 * (jj + 1)], g_sb[:, lo : lo + 128], ident_f[:])
-
-        def amm():
-            for I in range(4):
-                a_ps[(1, I)] = bank(4 + I, [P, 512], F32, "a1_%d" % I)
-                second(a_ps[(1, I)], "a", I, 0)
-                second(a_ps[(1, I)], "a", I, 1)
-
-        for step in SEQ0:
-            if step[0] == "u":
-                filler(99, int(step[1]))
-            elif step[0] == "f":
-                finish(0, int(step[1]))
-            elif step == "M":
-                mean_out(1)
-                stage1(1, 0)
-                stage1(1, 1)
-            elif step[0] == "p":
-                proj_quant(int(step[1]))
-            elif step[0] == "z":
-                zsig(int(step[1]))
-        amm()
+        add_chunk(1)
+        mean_out(1)
+        first_matmul(1, 0)
+        first_matmul(1, 1)
+        add_chunk(2)
+        proj_out(0)
+        proj_out(1)
+        add_chunk(3)
+        second_half_gate(0)
+        second_half_gate(1)
+        finish(0, 0)
+        second_half_gate(2)
+        finish(0, 1)
+        second_half_gate(3)
+        finish(0, 2)
+        finish(0, 3)
         for I in range(4):
-            gate(1, 0, I)
-            gate(1, 1, I)
-        add_slot(1, 0)
-        for l in range(L):
-            if l + 1 < L:
-                add_slot(1, l + 1)
+            add_ps[(1, I)] = bank(4 + I, [P, CHUNK], F32, "a1_%d" % I)
+            second_matmul(add_ps[(1, I)], "a", I)
+        for I in range(4):
+            multiply(1, 0, I)
+            multiply(1, 1, I)
+        add_row(0)
+        for l in range(ROWS):
+            if l + 1 < ROWS:
+                add_row(l + 1)
             finish(1, l)

from contextlib import ExitStack

import concourse.masks as masks
import concourse.mybir as mybir

FLOPS = 2 * 128 * 2048 * 1024 * 3

F32 = mybir.dt.float32
BF16 = mybir.dt.bfloat16
U32 = mybir.dt.uint32
U8 = mybir.dt.uint8
FP8X4 = mybir.dt.float8_e4m3fn_x4
ALU = mybir.AluOpType
ACT = mybir.ActivationFunctionType

P = 128
D = 2048
ROWS = 4
CHUNK = 512
LN_EPS = 1e-5
STEPS = 16
LAST_PIECES = 4

SLOT_OF = {
    "k0": 0, "y00": 0,
    "k1": 1, "y01": 1,
    "x0": 2, "a0": 2, "y10": 2,
    "x1": 3, "a1": 3, "y11": 3,
    "e0": 4, "x2": 4,
    "e1": 5, "x3": 5,
}
ADD_BANK = [2, 3, 4, 5]


def tile_ultralightweightmemory_pa_kernel(
    tc, interface, memory, W_write_key, W_write_erase, W_write_add, out
):
    nc = tc.nc
    with ExitStack() as ctx:
        const = ctx.enter_context(tc.tile_pool(name="const", bufs=1))
        keep = ctx.enter_context(tc.tile_pool(name="keep", bufs=1))
        slots = ctx.enter_context(tc.tile_pool(name="slots", bufs=1))
        grouped = ctx.enter_context(tc.tile_pool(name="grouped", bufs=4))
        psum = ctx.enter_context(tc.psum_pool(name="psum", bufs=1))
        ctx.enter_context(tc.manual_schedule())

        def bank(n, shape, dtype, name):
            return psum.tile(shape, dtype, tag="bank%d" % n, name=name)

        x_v = interface.rearrange("b s d -> (b s) d").rearrange("(T p i) d -> T p (i d)", p=P, i=2)
        wk_v = W_write_key.rearrange("(j p e) d -> j p (e d)", p=P, e=2)
        w2_v = {
            "e": W_write_erase.rearrange("(I h p c) r -> I p h (c r)", h=2, p=P, c=2),
            "a": W_write_add.rearrange("(I h p c) r -> I p h (c r)", h=2, p=P, c=2),
        }
        mem_v = memory.rearrange("b (u l) n -> (b u) (l n)", u=2)
        out_v = out.rearrange("b (u l) n -> (b u) (l n)", u=2)

        mem_sb = [keep.tile([P, ROWS * D], BF16, name="mem%d" % half) for half in range(2)]
        gate_sb = keep.tile([P, D], F32)
        squares = keep.tile([P, D], BF16)
        words = {}
        scales = {}
        for kind in "kea":
            words[kind] = keep.tile([P, 4096], U32, name="words_%s" % kind, align_bytes=64)
            scales[kind] = keep.tile([P, 4096], U8, name="scales_%s" % kind, align_bytes=64)
        mean_bf = keep.tile([P, 2048], BF16, align_bytes=64)
        mean_words = keep.tile([P, 512], U32, align_bytes=64)
        mean_scales = keep.tile([P, 512], U8, align_bytes=64)
        proj_bf = keep.tile([P, 1024], BF16, align_bytes=64)
        proj_words = keep.tile([P, 256], U32, align_bytes=64)
        proj_scales = keep.tile([P, 256], U8, align_bytes=64)
        part_sums = keep.tile([P, 2 * ROWS, 4], F32)
        neg_sum = keep.tile([P, 2 * ROWS], F32)
        neg_mean = keep.tile([P, 2 * ROWS], F32)
        sq_sum = keep.tile([P, 2 * ROWS], F32)
        var_eps = keep.tile([P, 2 * ROWS], F32)
        rstd = keep.tile([P, 2 * ROWS], F32)
        table_warm = keep.tile([P, 1], F32)

        raw = {}
        slot_tile = {}

        def load(kind, idx):
            if kind == "m":
                half, part = divmod(idx, 2)
                cols = slice(2 * D * part, 2 * D * (part + 1))
                nc.sync.dma_start(out=mem_sb[half][:, cols], in_=mem_v[P * half : P * (half + 1), cols])
                return
            if idx % 2 == 0:
                slot_tile[(kind, idx // 2)] = slots.tile(
                    [P, 8192], BF16, tag="slot%d" % SLOT_OF["%s%d" % (kind, idx // 2)], name="raw_%s%d" % (kind, idx // 2)
                )
            t = slot_tile[(kind, idx // 2)][:, 4096 * (idx % 2) : 4096 * (idx % 2 + 1)]
            if kind == "k":
                nc.sync.dma_start(out=t, in_=wk_v[idx])
            elif kind == "x":
                nc.sync.dma_start(out=t, in_=x_v[idx])
            else:
                nc.sync.dma_start(out=t.rearrange("p (h x) -> p h x", h=2), in_=w2_v[kind][idx])
            raw[(kind, idx)] = t

        for i in range(4):
            load("k", i)
        for i in range(4):
            load("x", i)
        for i in range(4):
            load("e", i)

        ident_f = const.tile([P, P], F32)
        masks.make_identity(nc, ident_f[:])
        ident_b = const.tile([P, P], BF16)
        masks.make_identity(nc, ident_b[:])
        member = const.tile([P, 16], F32)
        nc.vector.tensor_reduce(
            out=member[:], in_=ident_f[:].rearrange("p (n s) -> p n s", s=8), axis=mybir.AxisListType.X, op=ALU.add
        )
        averager = const.tile([P, 16], BF16)
        nc.vector.tensor_scalar_mul(out=averager[:], in0=member[:], scalar1=1.0 / 16.0)
        minus_half = const.tile([P, 1], F32)
        nc.vector.memset(minus_half[:], -0.5)
        nc.scalar.activation(out=table_warm[:], in_=minus_half[:], func=ACT.Sigmoid)

        def copy_out(engine, dst, src):
            if engine == "v":
                nc.vector.tensor_copy(out=dst, in_=src)
            else:
                nc.scalar.copy(out=dst, in_=src)

        def quantise(words_ap, scales_ap, in_ap):
            nc.vector.quantize_mx(out=words_ap.bitcast(FP8X4), scales=scales_ap, in_=in_ap)

        waiting = []

        def quantise_waiting(keep_back):
            while len(waiting) > keep_back:
                waiting.pop(0)()

        turn = {"n": 0}

        def transpose_bank(shape, dtype, name, banks=4):
            turn["n"] += 1
            return bank(8 - banks + turn["n"] % banks, shape, dtype, name)

        def prepare_key(j, e):
            loaded = raw[("k", j)]
            ce = 2 * j + e
            group = grouped.tile([P, 2048], BF16, tag="grp", name="gk%d" % ce, align_bytes=64)
            for g in range(4):
                tp = transpose_bank([P, 4, P], BF16, "tpk%d_%d" % (ce, g))
                for t in range(4):
                    d0 = e * D + 512 * g + 128 * t
                    nc.tensor.transpose(tp[:, t, :], loaded[:, d0 : d0 + 128], ident_b[:])
                copy_out(
                    "vs"[g % 2],
                    group[:, 512 * g : 512 * (g + 1)].rearrange("p (c t) -> p c t", t=4),
                    tp[:].rearrange("p t c -> p c t"),
                )
            cols = slice(512 * ce, 512 * (ce + 1))
            waiting.append(lambda: quantise(words["k"][:, cols], scales["k"][:, cols], group[:]))
            quantise_waiting(1)

        mean_ps = {}

        def mean_chunk(T):
            half, Tl = divmod(T, 4)
            if Tl == 0:
                mean_ps[half] = [bank(z, [P, 8, 64], F32, "mean%d_%d" % (half, z)) for z in range(2)]
            xt = raw[("x", T)]
            for c in range(16):
                for i in range(2):
                    nc.tensor.matmul(
                        mean_ps[half][c // 8][:, c % 8, 16 * Tl : 16 * (Tl + 1)],
                        lhsT=xt[:, i * D + 128 * c : i * D + 128 * (c + 1)],
                        rhs=averager[:],
                        start=(i == 0),
                        stop=(i == 1),
                    )

        def mean_out(half):
            for z in range(2):
                for g in (z, 2 + z):
                    src = mean_ps[half][g // 2][:, 4 * (g % 2) : 4 * (g % 2) + 4, :]
                    copy_out(
                        "vs"[g // 2],
                        mean_bf[:, 512 * g : 512 * (g + 1)].rearrange("p (b u t) -> p b u t", u=2, t=4),
                        src.rearrange("p t b -> p b t").unsqueeze(2).to_broadcast([P, 64, 2, 4]),
                    )
            quantise(mean_words[:, 0:256], mean_scales[:, 0:256], mean_bf[:, 0:1024])
            quantise(mean_words[:, 256:512], mean_scales[:, 256:512], mean_bf[:, 1024:2048])

        proj_ps = {}

        def first_matmul(half, G):
            pj = bank(2 + 4 * half + G, [P, 4, P], F32, "pj%d_%d" % (half, G))
            proj_ps[G] = pj
            for t in range(4):
                ce = 4 * G + t
                for g in range(4):
                    lo = 512 * ce + 128 * g
                    nc.tensor.matmul_mx(
                        out=pj[:, t, :],
                        lhsT=words["k"][:, lo : lo + 128].bitcast(FP8X4),
                        lhsT_scale=scales["k"][:, lo : lo + 128],
                        rhs=mean_words[:, 128 * g : 128 * (g + 1)].bitcast(FP8X4),
                        rhs_scale=mean_scales[:, 128 * g : 128 * (g + 1)],
                        start=(g == 0),
                        stop=(g == 3),
                    )

        def proj_out(G):
            copy_out(
                "v",
                proj_bf[:, 512 * G : 512 * (G + 1)].rearrange("p (b t) -> p b t", t=4),
                proj_ps[G][:].rearrange("p t b -> p b t"),
            )
            cols = slice(128 * G, 128 * (G + 1))
            quantise(proj_words[:, cols], proj_scales[:, cols], proj_bf[:, 512 * G : 512 * (G + 1)])

        chunks = [("e", I) for I in range(4)] + [("a", I) for I in range(4)]

        def prepare(step):
            kind, I = chunks[step // 2]
            h = step % 2
            r_pairs = raw[(kind, I)].bitcast(F32)
            group = grouped.tile([P, 2048], BF16, tag="grp", name="gw%d" % step, align_bytes=64)
            group_r_pairs = group[:].bitcast(F32)
            for G in range(2):
                tp = transpose_bank([P, 2, 2, P], F32, "tpw%d_%d" % (step, G), 2 if step >= STEPS - 2 else 4)
                for c in range(2):
                    for u in range(2):
                        w0 = (h * 2 + c) * 512 + 256 * G + 128 * u
                        nc.tensor.transpose(tp[:, c, u, :], r_pairs[:, w0 : w0 + 128], ident_f[:])
                copy_out(
                    "s",
                    group_r_pairs[:, 512 * G : 512 * (G + 1)].rearrange("q (p c u) -> q p c u", c=2, u=2),
                    tp[:].rearrange("q c u p -> q p c u"),
                )
            if kind == "e" and step % 4 == 3:
                load("x", 3 + I)
                load("x", 4 + I)
                if I == 3:
                    load("m", 2)
                    load("m", 3)
            cols = slice(512 * (2 * I + h), 512 * (2 * I + h + 1))
            waiting.append(lambda: quantise(words[kind][:, cols], scales[kind][:, cols], group[:]))

        def second_matmul(o_ps, kind, I):
            for h in range(2):
                for G in range(2):
                    lo = 512 * (2 * I + h) + 256 * G
                    nc.tensor.matmul_mx(
                        out=o_ps[:, 256 * h : 256 * (h + 1)],
                        lhsT=proj_words[:, 128 * G : 128 * (G + 1)].bitcast(FP8X4),
                        lhsT_scale=proj_scales[:, 128 * G : 128 * (G + 1)],
                        rhs=words[kind][:, lo : lo + 256].bitcast(FP8X4),
                        rhs_scale=scales[kind][:, lo : lo + 256],
                        start=(G == 0),
                        stop=(G == 1),
                    )

        add_ps = {}
        gate_ps = {}

        def first_half_products(kind, I):
            if kind == "e":
                o_ps = bank(I % 2, [P, CHUNK], F32, "o_e%d" % I)
                second_matmul(o_ps, kind, I)
                nc.scalar.activation(
                    out=gate_sb[:, CHUNK * I : CHUNK * (I + 1)], in_=o_ps[:], func=ACT.Sigmoid, scale=-1.0
                )
            else:
                add_ps[(0, I)] = bank(ADD_BANK[I], [P, CHUNK], F32, "o_a%d" % I)
                second_matmul(add_ps[(0, I)], kind, I)

        def second_half_gate(I):
            z_ps = bank(7, [P, 4, P], F32, "zt%d" % I)
            for jj in range(4):
                for G in range(2):
                    lo = 512 * (2 * I + jj // 2) + 256 * G + 128 * (jj % 2)
                    nc.tensor.matmul_mx(
                        out=z_ps[:, jj, :],
                        lhsT=words["e"][:, lo : lo + 128].bitcast(FP8X4),
                        lhsT_scale=scales["e"][:, lo : lo + 128],
                        rhs=proj_words[:, 128 * G : 128 * (G + 1)].bitcast(FP8X4),
                        rhs_scale=proj_scales[:, 128 * G : 128 * (G + 1)],
                        start=(G == 0),
                        stop=(G == 1),
                    )
            nc.scalar.activation(
                out=gate_sb[:, CHUNK * I : CHUNK * (I + 1)],
                in_=z_ps[:].rearrange("p j b -> p (j b)"),
                func=ACT.Sigmoid,
                scale=-1.0,
            )
            gate_ps[I] = bank(I, [P, CHUNK], F32, "gps%d" % I)
            for jj in range(4):
                lo = CHUNK * I + 128 * jj
                nc.tensor.transpose(gate_ps[I][:, 128 * jj : 128 * (jj + 1)], gate_sb[:, lo : lo + 128], ident_f[:])

        y_tile = {}

        def y_row(half, l):
            return y_tile[(half, l // 2)][:, D * (l % 2) : D * (l % 2 + 1)]

        def multiply(half, k, I):
            if (half, k) not in y_tile:
                y_tile[(half, k)] = slots.tile(
                    [P, 2 * D], F32, tag="slot%d" % SLOT_OF["y%d%d" % (half, k)], name="y%d_%d" % (half, k)
                )
            ns = slice(CHUNK * I, CHUNK * (I + 1))
            yv = y_tile[(half, k)][:].rearrange("p (l n) -> p l n", l=2)
            mv = mem_sb[half][:].rearrange("p (l n) -> p l n", l=ROWS)
            nc.vector.tensor_tensor(
                out=yv[:, :, ns],
                in0=mv[:, 2 * k : 2 * k + 2, ns],
                in1=(gate_sb[:, ns] if half == 0 else gate_ps[I][:]).unsqueeze(1).to_broadcast([P, 2, CHUNK]),
                op=ALU.mult,
            )

        def add(half, l, I):
            ym = y_row(half, l)[:, CHUNK * I : CHUNK * (I + 1)]
            nc.vector.scalar_tensor_tensor(
                out=ym,
                in0=ym,
                scalar=1.0,
                in1=add_ps[(half, I)][:],
                op0=ALU.mult,
                op1=ALU.add,
                accum_out=part_sums[:, ROWS * half + l, I : I + 1],
            )

        def total(first, count):
            nc.vector.tensor_reduce(
                out=neg_sum[:, first : first + count],
                in_=part_sums[:, first : first + count, :],
                axis=mybir.AxisListType.X,
                op=ALU.add,
                negate=True,
            )

        def add_chunk(I):
            for l in range(ROWS):
                add(0, l, I)
            if I == 3:
                total(0, ROWS)

        def add_row(l):
            for I in range(4):
                add(1, l, I)
            total(ROWS + l, 1)

        def finish(half, l):
            j = ROWS * half + l
            col = slice(j, j + 1)
            ym = y_row(half, l)
            hbm_rows = slice(P * half, P * (half + 1))
            nc.scalar.activation(
                out=squares[:], in_=ym, func=ACT.Square, bias=neg_sum[:, col], scale=float(D), accum_out=sq_sum[:, col]
            )
            nc.scalar.activation(out=neg_mean[:, col], in_=neg_sum[:, col], func=ACT.Copy, scale=1.0 / D)
            nc.gpsimd.tensor_scalar(
                out=var_eps[:, col],
                in0=sq_sum[:, col],
                scalar1=1.0 / (D * D * D),
                scalar2=LN_EPS,
                op0=ALU.mult,
                op1=ALU.add,
            )
            nc.gpsimd.tensor_tensor(out=rstd[:, col], in0=var_eps[:, col], in1=minus_half[:], op=ALU.pow)
            if j >= 2 * ROWS - 2:
                w = D // LAST_PIECES
                for z in range(LAST_PIECES):
                    yz = ym[:, w * z : w * (z + 1)]
                    nc.vector.tensor_scalar(
                        out=yz, in0=yz, scalar1=neg_mean[:, col], scalar2=rstd[:, col], op0=ALU.add, op1=ALU.mult
                    )
                    nc.sync.dma_start(out=out_v[hbm_rows, D * l + w * z : D * l + w * (z + 1)], in_=yz)
            else:
                nc.gpsimd.tensor_scalar(
                    out=ym, in0=ym, scalar1=neg_mean[:, col], scalar2=rstd[:, col], op0=ALU.add, op1=ALU.mult
                )
                nc.sync.dma_start(out=out_v[hbm_rows, D * l : D * (l + 1)], in_=ym)

        for j in range(4):
            prepare_key(j, 0)
            prepare_key(j, 1)
        for T in range(4):
            mean_chunk(T)
            if T % 2 == 1:
                if T == 1:
                    load("m", 0)
                    load("m", 1)
                load("a", T - 1)
                load("a", T)
        quantise_waiting(0)
        mean_out(0)
        for step in range(2):
            prepare(step)
            quantise_waiting(1)
        first_matmul(0, 0)
        proj_out(0)
        quantise_waiting(0)
        first_matmul(0, 1)
        proj_out(1)

        for step in range(2, STEPS + 2):
            if step < STEPS:
                prepare(step)
                quantise_waiting(1)
            else:
                quantise_waiting(0)
            if step % 2 == 1:
                kind, I = chunks[(step - 3) // 2]
                first_half_products(kind, I)
            if step >= STEPS - 2:
                mean_chunk(step - STEPS + 6)
            if 4 <= step < 12:
                multiply(0, step % 2, (step - 4) // 2)
            if step == 12:
                add_chunk(0)

        add_chunk(1)
        mean_out(1)
        first_matmul(1, 0)
        first_matmul(1, 1)
        add_chunk(2)
        proj_out(0)
        proj_out(1)
        add_chunk(3)
        second_half_gate(0)
        second_half_gate(1)
        finish(0, 0)
        second_half_gate(2)
        finish(0, 1)
        second_half_gate(3)
        finish(0, 2)
        finish(0, 3)
        for I in range(4):
            add_ps[(1, I)] = bank(4 + I, [P, CHUNK], F32, "a1_%d" % I)
            second_matmul(add_ps[(1, I)], "a", I)
        for I in range(4):
            multiply(1, 0, I)
            multiply(1, 1, I)
        add_row(0)
        for l in range(ROWS):
            if l + 1 < ROWS:
                add_row(l + 1)
            finish(1, l)
